import numpy as np
import ml_dtypes


def mxq(x, axis, fmt="e4m3"):
    dtype, down = {"e4m3": (ml_dtypes.float8_e4m3fn, 7), "e5m2": (ml_dtypes.float8_e5m2, 14)}[fmt]
    v = np.moveaxis(np.asarray(x, np.float32).astype(ml_dtypes.bfloat16).astype(np.float64), axis, -1)
    blocks = v.reshape(v.shape[:-1] + (-1, 32))
    amax = np.abs(blocks).max(-1, keepdims=True)
    byte = np.maximum(np.where(amax > 0, np.frexp(amax)[1] - 1 + 127, 0) - down, 1)
    scale = np.exp2(byte - 127.0)
    codes = (blocks / scale).astype(np.float32).astype(dtype).astype(np.float64)
    return np.moveaxis((codes * scale).reshape(v.shape), -1, axis)


WIDE = False


def mx_kscale(k):
    if not WIDE:
        return np.ones(k)
    levels = np.array([10, -10, 5, -5, 0])
    if k % 512:
        return np.exp2(np.random.permutation(np.resize(levels, k // 32))).repeat(32)
    a = np.empty((k // 512, 16))
    for p in range(k // 512):
        a[p, :8] = np.random.permutation(np.resize(levels, 8))
        for g in range(8):
            far = levels[np.abs(levels - a[p, g]) >= 10]
            a[p, g + 8] = far[np.random.randint(len(far))]
    return np.exp2(a.ravel()).repeat(32)


BF16 = ml_dtypes.bfloat16


def bf(x):
    return np.asarray(x, np.float32).astype(BF16)


def f64(x):
    return np.asarray(x).astype(np.float64)


B, C, CK, H, W = 2, 1024, 512, 32, 32
N = H * W
EPS = 1e-5


def setup_inputs():
    s = mx_kscale(N)
    u = s / s.max()
    v = s.min() / s
    r = u.mean()
    fg0 = bf(np.random.uniform(size=(B, N, N)))
    return {
        "sim_fg": bf(np.random.standard_normal((B, N, N)) * f64(fg0)),
        "fg_sim": bf(f64(fg0) * u[None, None, :]),
        "bg_sim": bf(np.random.uniform(size=(B, N, N)) * 2.0 / N * u[None, None, :] / r),
        "x": bf(np.random.standard_normal((B, C, H, W)) * v.reshape(1, 1, H, W)),
        "gamma": bf(np.sqrt(N) * 0.3 * (1.0 + 0.1 * np.random.standard_normal(1)) * r * s.max() / s.min()),
    }


def reference(sim_fg, fg_sim, bg_sim, x, gamma):
    sim = f64(sim_fg)
    fg = f64(fg_sim)
    xf = f64(x).reshape(B, C, N)
    min_v = sim.min(-1, keepdims=True)
    x1 = (sim - min_v) * fg
    attn = x1 / (x1.sum(-1, keepdims=True) + EPS) + f64(bg_sim)
    value = xf.transpose(0, 2, 1)
    context = mxq(attn, 2, "e4m3") @ mxq(value, 1, "e4m3")
    context = context.transpose(0, 2, 1).reshape(B, C, H, W)
    return f64(gamma)[0] * context + f64(x)

@@ -1,0 +1,240 @@
+from contextlib import ExitStack
+
+import concourse.mybir as mybir
+from concourse.masks import make_identity
+
+F32 = mybir.dt.float32
+BF16 = mybir.dt.bfloat16
+U32 = mybir.dt.uint32
+U8 = mybir.dt.uint8
+FP8X4 = mybir.dt.float8_e4m3fn_x4
+ALU = mybir.AluOpType
+ACT = mybir.ActivationFunctionType
+
+P = 128
+BATCH = 2
+PIXELS = 1024
+CHANNELS = 1024
+EPS = 1e-5
+PACK = 4
+K_PASS = P * PACK
+PASSES = PIXELS // K_PASS
+PLANES = 2
+UNIT = 512
+HALVES = PIXELS // UNIT
+ROW_TILES = UNIT // P
+PAIR = 2
+PAIRS = BATCH * HALVES * ROW_TILES // PAIR
+C_TILES = CHANNELS // P
+QUAD = 4
+AHEAD = 3
+
+FLOPS = 2 * BATCH * PIXELS * PIXELS * CHANNELS
+
+
+def tile_sgan_pb_kernel(tc, sim_fg, fg_sim, bg_sim, x, gamma, out):
+    nc = tc.nc
+
+    sim_rows = sim_fg.rearrange("b (h p j) m -> b h p j m", h=HALVES, j=ROW_TILES)
+    fg_rows = fg_sim.rearrange("b (h p j) m -> b h p j m", h=HALVES, j=ROW_TILES)
+    bg_rows = bg_sim.rearrange("b (h p j) m -> b h p j m", h=HALVES, j=ROW_TILES)
+    x_rows = x.rearrange("b (p t) r s -> b p t (r s)", t=C_TILES)
+    out_rows = out.rearrange("b (p t) r s -> b p t (r s)", t=C_TILES)
+
+    with ExitStack() as ctx:
+        const = ctx.enter_context(tc.tile_pool(name="const", bufs=1))
+        rows = ctx.enter_context(tc.tile_pool(name="rows", bufs=AHEAD + 1))
+        image = ctx.enter_context(tc.tile_pool(name="image", bufs=BATCH))
+        work = ctx.enter_context(tc.tile_pool(name="work", bufs=4))
+        stats = ctx.enter_context(tc.tile_pool(name="stats", bufs=3))
+        packed = ctx.enter_context(tc.tile_pool(name="packed", bufs=2))
+        turned = ctx.enter_context(tc.psum_pool(name="turned", bufs=4))
+        sums = ctx.enter_context(tc.psum_pool(name="sums", bufs=4))
+
+        identity = const.tile([P, P], F32, name="identity")
+        make_identity(nc, identity[:])
+        gamma_bf16 = const.tile([P, 1], BF16, name="gamma_bf16")
+        nc.scalar.dma_start(out=gamma_bf16[:], in_=gamma.partition_broadcast(P))
+        gamma_f32 = const.tile([P, 1], F32, name="gamma_f32")
+        nc.vector.tensor_copy(out=gamma_f32[:], in_=gamma_bf16[:])
+
+        def place(k):
+            b, rest = divmod(k, HALVES * ROW_TILES // PAIR)
+            h, q = divmod(rest, ROW_TILES // PAIR)
+            return b, h, q
+
+        def load_pair(k):
+            b, h, q = place(k)
+            js = slice(PAIR * q, PAIR * q + PAIR)
+            sim_t = rows.tile([P, PAIR, PIXELS], BF16, name="sim_t")
+            nc.sync.dma_start(out=sim_t[:], in_=sim_rows[b, h, :, js, :])
+            fg_t = rows.tile([P, PAIR, PIXELS], BF16, name="fg_t")
+            nc.sync.dma_start(out=fg_t[:], in_=fg_rows[b, h, :, js, :])
+            bg_t = rows.tile([P, PAIR, PIXELS], BF16, name="bg_t")
+            nc.sync.dma_start(out=bg_t[:], in_=bg_rows[b, h, :, js, :])
+            return sim_t, fg_t, bg_t
+
+        def load_channels(b, x_t, first):
+            for t in range(first, first + QUAD, PAIR):
+                nc.sync.dma_start(out=x_t[:, t : t + PAIR, :], in_=x_rows[b, :, t : t + PAIR, :])
+
+        def turn(source, grouped_words):
+            words = source.bitcast(F32)
+            bank = turned.tile([P, PASSES, PLANES, P], F32, name="bank")
+            for g in range(PASSES):
+                for u in range(PLANES):
+                    first = g * PLANES * P
+                    nc.tensor.transpose(
+                        bank[:, g, u, :], words[:, first + u : first + PLANES * P : PLANES], identity[:]
+                    )
+            nc.scalar.copy(out=grouped_words, in_=bank[:].rearrange("k g u r -> k g r u"))
+
+        def by_block(row):
+            return row.rearrange("n (g k t) -> n g t k", k=P, t=PACK)
+
+        def normalise_pair(tiles, q, a_grouped):
+            sim_t, fg_t, bg_t = tiles
+            lowest = stats.tile([P, PAIR], F32, name="lowest")
+            total = stats.tile([P, PAIR], F32, name="total")
+            divisor = stats.tile([P, PAIR], F32, name="divisor")
+            inverse = stats.tile([P, PAIR], F32, name="inverse")
+            for i in range(PAIR):
+                unread = work.tile([P, PIXELS], BF16, name="unread", bufs=2)
+                nc.vector.tensor_scalar(
+                    out=unread[:],
+                    in0=sim_t[:, i, :],
+                    scalar1=1.0,
+                    scalar2=None,
+                    op0=ALU.mult,
+                    op1=ALU.min,
+                    accum_out=lowest[:, i : i + 1],
+                )
+            masked = []
+            for i in range(PAIR):
+                x1 = work.tile([P, PIXELS], F32, name="x1")
+                nc.vector.scalar_tensor_tensor(
+                    out=x1[:],
+                    in0=sim_t[:, i, :],
+                    scalar=lowest[:, i : i + 1],
+                    in1=fg_t[:, i, :],
+                    op0=ALU.subtract,
+                    op1=ALU.mult,
+                    accum_out=total[:, i : i + 1],
+                )
+                masked.append(x1)
+            nc.vector.tensor_scalar_add(out=divisor[:], in0=total[:], scalar1=EPS)
+            nc.vector.reciprocal(out=inverse[:], in_=divisor[:])
+            for i in range(PAIR):
+                bg_f32 = work.tile([P, PASSES * PACK, P], F32, name="bg_f32")
+                nc.scalar.copy(
+                    out=bg_f32[:].rearrange("n (g t) k -> n g t k", t=PACK), in_=by_block(bg_t[:, i, :])
+                )
+                scaled = work.tile([P, PASSES * PACK, P], F32, name="scaled")
+                nc.scalar.activation(
+                    out=scaled[:].rearrange("n (g t) k -> n g t k", t=PACK),
+                    in_=by_block(masked[i][:]),
+                    func=ACT.Copy,
+                    scale=inverse[:, i : i + 1],
+                )
+                first = (PAIR * q + i) * P
+                for g in range(PASSES):
+                    bank = turned.tile([P, PACK, P], F32, name="bank")
+                    for t in range(PACK):
+                        block = g * PACK + t
+                        nc.tensor.matmul(
+                            out=bank[:, t, :],
+                            lhsT=scaled[:, block, :],
+                            rhs=identity[:],
+                            is_transpose=True,
+                            start=True,
+                            stop=False,
+                        )
+                        nc.tensor.matmul(
+                            out=bank[:, t, :],
+                            lhsT=bg_f32[:, block, :],
+                            rhs=identity[:],
+                            is_transpose=True,
+                            start=False,
+                            stop=True,
+                        )
+                    nc.scalar.copy(
+                        out=a_grouped[:, g, first : first + P, :], in_=bank[:].rearrange("k t r -> k r t")
+                    )
+
+        def quantise_channels(x_t, x_codes, x_scales):
+            for first in range(0, C_TILES, QUAD):
+                x_grouped = packed.tile([P, QUAD, PASSES, P, PACK], BF16, name="x_grouped", align_bytes=64)
+                x_words = x_grouped[:].bitcast(F32)
+                for i in range(QUAD):
+                    turn(x_t[:, first + i, :], x_words[:, i, :, :, :])
+                nc.vector.quantize_mx(
+                    out=x_codes[:, first : first + QUAD, :, :].rearrange("k t g c -> k (t g c)").bitcast(FP8X4),
+                    scales=x_scales[:, first : first + QUAD, :, :].rearrange("k t g c -> k (t g c)"),
+                    in_=x_grouped[:].rearrange("k t g c v -> k (t g c v)"),
+                )
+
+        def multiply_unit(b, h, a_grouped, x_t, x_codes, x_scales):
+            a_codes = packed.tile([P, PASSES, UNIT], U32, name="a_codes", align_bytes=64)
+            a_scales = packed.tile([P, PASSES, UNIT], U8, name="a_scales", align_bytes=64)
+            nc.vector.quantize_mx(
+                out=a_codes[:].rearrange("k g n -> k (g n)").bitcast(FP8X4),
+                scales=a_scales[:].rearrange("k g n -> k (g n)"),
+                in_=a_grouped[:].rearrange("k g n v -> k (g n v)"),
+            )
+            pixels = slice(h * UNIT, h * UNIT + UNIT)
+            for first in range(0, C_TILES, PAIR):
+                result = work.tile([P, PAIR, UNIT], F32, name="result")
+                for i in range(PAIR):
+                    t = first + i
+                    context = sums.tile([P, UNIT], F32, name="context")
+                    for g in range(PASSES):
+                        nc.tensor.matmul_mx(
+                            out=context[:],
+                            lhsT=x_codes[:, t, g, :].bitcast(FP8X4),
+                            lhsT_scale=x_scales[:, t, g, :],
+                            rhs=a_codes[:, g, :].bitcast(FP8X4),
+                            rhs_scale=a_scales[:, g, :],
+                            start=(g == 0),
+                            stop=(g == PASSES - 1),
+                        )
+                    nc.vector.scalar_tensor_tensor(
+                        out=result[:, i, :].rearrange("c (p j) -> c p j", j=ROW_TILES),
+                        in0=context[:].rearrange("c (j p) -> c p j", j=ROW_TILES),
+                        scalar=gamma_f32[:, 0:1],
+                        in1=x_t[:, t, pixels].rearrange("c (p j) -> c p j", j=ROW_TILES),
+                        op0=ALU.mult,
+                        op1=ALU.add,
+                    )
+                nc.sync.dma_start(out=out_rows[b, :, first : first + PAIR, pixels], in_=result[:])
+
+        loaded = {}
+        x_tiles = {}
+
+        def issue_loads(k):
+            if k >= PAIRS:
+                return
+            b, h, q = place(k)
+            loaded[k] = load_pair(k)
+            if h == 0:
+                if q == 0:
+                    x_tiles[b] = image.tile([P, C_TILES, PIXELS], BF16, name="x_t")
+                load_channels(b, x_tiles[b], q * QUAD)
+
+        for k in range(AHEAD):
+            issue_loads(k)
+
+        x_packed = {}
+        a_grouped = None
+        for k in range(PAIRS):
+            b, h, q = place(k)
+            issue_loads(k + AHEAD)
+            if q == 0:
+                a_grouped = packed.tile([P, PASSES, UNIT, PACK], BF16, name="a_grouped", align_bytes=64)
+            normalise_pair(loaded[k], q, a_grouped)
+            if h == 0 and q == 0:
+                x_codes = image.tile([P, C_TILES, PASSES, P], U32, name="x_codes", align_bytes=64)
+                x_scales = image.tile([P, C_TILES, PASSES, P], U8, name="x_scales", align_bytes=64)
+                quantise_channels(x_tiles[b], x_codes, x_scales)
+                x_packed[b] = (x_codes, x_scales)
+            if q == ROW_TILES // PAIR - 1:
+                multiply_unit(b, h, a_grouped, x_tiles[b], x_packed[b][0], x_packed[b][1])

@@ -89,8 +89,11 @@ def tile_sgan_pb_kernel(tc, sim_fg, fg_sim, bg_sim, x, gamma, out):
                     )
             nc.scalar.copy(out=grouped_words, in_=bank[:].rearrange("k g u r -> k g r u"))
 
-        def by_block(row):
-            return row.rearrange("n (g k t) -> n g t k", k=P, t=PACK)
+        def by_word(row):
+            return row.rearrange("n (g k t) -> n g k t", k=P, t=PACK)
+
+        def into_blocks(blocks):
+            return blocks.rearrange("n (g t) k -> n g k t", t=PACK)
 
         def normalise_pair(tiles, q, a_grouped):
             sim_t, fg_t, bg_t = tiles
@@ -127,12 +130,12 @@ def tile_sgan_pb_kernel(tc, sim_fg, fg_sim, bg_sim, x, gamma, out):
             for i in range(PAIR):
                 bg_f32 = work.tile([P, PASSES * PACK, P], F32, name="bg_f32")
                 nc.scalar.copy(
-                    out=bg_f32[:].rearrange("n (g t) k -> n g t k", t=PACK), in_=by_block(bg_t[:, i, :])
+                    out=into_blocks(bg_f32[:]), in_=by_word(bg_t[:, i, :])
                 )
                 scaled = work.tile([P, PASSES * PACK, P], F32, name="scaled")
                 nc.scalar.activation(
-                    out=scaled[:].rearrange("n (g t) k -> n g t k", t=PACK),
-                    in_=by_block(masked[i][:]),
+                    out=into_blocks(scaled[:]),
+                    in_=by_word(masked[i][:]),
                     func=ACT.Copy,
                     scale=inverse[:, i : i + 1],
                 )

@@ -27,6 +27,7 @@ PAIR = 2
 PAIRS = BATCH * HALVES * ROW_TILES // PAIR
 C_TILES = CHANNELS // P
 QUAD = 4
+MATMUL_TILES = 3
 AHEAD = 3
 
 FLOPS = 2 * BATCH * PIXELS * PIXELS * CHANNELS
@@ -53,6 +54,8 @@ def tile_sgan_pb_kernel(tc, sim_fg, fg_sim, bg_sim, x, gamma, out):
 
         identity = const.tile([P, P], F32, name="identity")
         make_identity(nc, identity[:])
+        identity_bf16 = const.tile([P, P], BF16, name="identity_bf16")
+        make_identity(nc, identity_bf16[:])
         gamma_bf16 = const.tile([P, 1], BF16, name="gamma_bf16")
         nc.scalar.dma_start(out=gamma_bf16[:], in_=gamma.partition_broadcast(P))
         gamma_f32 = const.tile([P, 1], F32, name="gamma_f32")
@@ -128,10 +131,11 @@ def tile_sgan_pb_kernel(tc, sim_fg, fg_sim, bg_sim, x, gamma, out):
             nc.vector.tensor_scalar_add(out=divisor[:], in0=total[:], scalar1=EPS)
             nc.vector.reciprocal(out=inverse[:], in_=divisor[:])
             for i in range(PAIR):
-                bg_f32 = work.tile([P, PASSES * PACK, P], F32, name="bg_f32")
-                nc.scalar.copy(
-                    out=into_blocks(bg_f32[:]), in_=by_word(bg_t[:, i, :])
-                )
+                j = PAIR * q + i
+                bg_f32 = None
+                if j >= MATMUL_TILES:
+                    bg_f32 = work.tile([P, PASSES * PACK, P], F32, name="bg_f32", bufs=2)
+                    nc.scalar.copy(out=into_blocks(bg_f32[:]), in_=by_word(bg_t[:, i, :]))
                 scaled = work.tile([P, PASSES * PACK, P], F32, name="scaled")
                 nc.scalar.activation(
                     out=into_blocks(scaled[:]),
@@ -139,7 +143,7 @@ def tile_sgan_pb_kernel(tc, sim_fg, fg_sim, bg_sim, x, gamma, out):
                     func=ACT.Copy,
                     scale=inverse[:, i : i + 1],
                 )
-                first = (PAIR * q + i) * P
+                first = j * P
                 for g in range(PASSES):
                     bank = turned.tile([P, PACK, P], F32, name="bank")
                     for t in range(PACK):
@@ -152,14 +156,23 @@ def tile_sgan_pb_kernel(tc, sim_fg, fg_sim, bg_sim, x, gamma, out):
                             start=True,
                             stop=False,
                         )
-                        nc.tensor.matmul(
-                            out=bank[:, t, :],
-                            lhsT=bg_f32[:, block, :],
-                            rhs=identity[:],
-                            is_transpose=True,
-                            start=False,
-                            stop=True,
-                        )
+                        if bg_f32 is None:
+                            nc.tensor.matmul(
+                                out=bank[:, t, :],
+                                lhsT=bg_t[:, i, g * K_PASS + t : (g + 1) * K_PASS : PACK],
+                                rhs=identity_bf16[:],
+                                start=False,
+                                stop=True,
+                            )
+                        else:
+                            nc.tensor.matmul(
+                                out=bank[:, t, :],
+                                lhsT=bg_f32[:, block, :],
+                                rhs=identity[:],
+                                is_transpose=True,
+                                start=False,
+                                stop=True,
+                            )
                     nc.scalar.copy(
                         out=a_grouped[:, g, first : first + P, :], in_=bank[:].rearrange("k t r -> k r t")
                     )

@@ -20,15 +20,14 @@ PACK = 4
 K_PASS = P * PACK
 PASSES = PIXELS // K_PASS
 PLANES = 2
-UNIT = 512
-HALVES = PIXELS // UNIT
-ROW_TILES = UNIT // P
-PAIR = 2
-PAIRS = BATCH * HALVES * ROW_TILES // PAIR
+TILES = 2
+UNIT = TILES * P
+UNITS = PIXELS // UNIT
+STORE_UNITS = 2
 C_TILES = CHANNELS // P
-QUAD = 4
-MATMUL_TILES = 3
-AHEAD = 3
+PAIR = 2
+C_PAIRS = C_TILES // PAIR
+VECTOR_EVERY = 4
 
 FLOPS = 2 * BATCH * PIXELS * PIXELS * CHANNELS
 
@@ -36,18 +35,18 @@ FLOPS = 2 * BATCH * PIXELS * PIXELS * CHANNELS
 def tile_sgan_pb_kernel(tc, sim_fg, fg_sim, bg_sim, x, gamma, out):
     nc = tc.nc
 
-    sim_rows = sim_fg.rearrange("b (h p j) m -> b h p j m", h=HALVES, j=ROW_TILES)
-    fg_rows = fg_sim.rearrange("b (h p j) m -> b h p j m", h=HALVES, j=ROW_TILES)
-    bg_rows = bg_sim.rearrange("b (h p j) m -> b h p j m", h=HALVES, j=ROW_TILES)
+    sim_rows = sim_fg.rearrange("b (s j p) m -> (b s) p j m", s=UNITS, j=TILES)
+    fg_rows = fg_sim.rearrange("b (s j p) m -> (b s) p j m", s=UNITS, j=TILES)
+    bg_rows = bg_sim.rearrange("b (s j p) m -> (b s) p j m", s=UNITS, j=TILES)
     x_rows = x.rearrange("b (p t) r s -> b p t (r s)", t=C_TILES)
     out_rows = out.rearrange("b (p t) r s -> b p t (r s)", t=C_TILES)
 
     with ExitStack() as ctx:
         const = ctx.enter_context(tc.tile_pool(name="const", bufs=1))
-        rows = ctx.enter_context(tc.tile_pool(name="rows", bufs=AHEAD + 1))
+        rows = ctx.enter_context(tc.tile_pool(name="rows", bufs=6))
         image = ctx.enter_context(tc.tile_pool(name="image", bufs=BATCH))
         work = ctx.enter_context(tc.tile_pool(name="work", bufs=4))
-        stats = ctx.enter_context(tc.tile_pool(name="stats", bufs=3))
+        stats = ctx.enter_context(tc.tile_pool(name="stats", bufs=4))
         packed = ctx.enter_context(tc.tile_pool(name="packed", bufs=2))
         turned = ctx.enter_context(tc.psum_pool(name="turned", bufs=4))
         sums = ctx.enter_context(tc.psum_pool(name="sums", bufs=4))
@@ -57,40 +56,59 @@ def tile_sgan_pb_kernel(tc, sim_fg, fg_sim, bg_sim, x, gamma, out):
         identity_bf16 = const.tile([P, P], BF16, name="identity_bf16")
         make_identity(nc, identity_bf16[:])
         gamma_bf16 = const.tile([P, 1], BF16, name="gamma_bf16")
-        nc.scalar.dma_start(out=gamma_bf16[:], in_=gamma.partition_broadcast(P))
         gamma_f32 = const.tile([P, 1], F32, name="gamma_f32")
-        nc.vector.tensor_copy(out=gamma_f32[:], in_=gamma_bf16[:])
 
-        def place(k):
-            b, rest = divmod(k, HALVES * ROW_TILES // PAIR)
-            h, q = divmod(rest, ROW_TILES // PAIR)
-            return b, h, q
+        row_tiles = {}
+        x_tiles = {}
+        x_packed = {}
+        results = {}
 
-        def load_pair(k):
-            b, h, q = place(k)
-            js = slice(PAIR * q, PAIR * q + PAIR)
-            sim_t = rows.tile([P, PAIR, PIXELS], BF16, name="sim_t")
-            nc.sync.dma_start(out=sim_t[:], in_=sim_rows[b, h, :, js, :])
-            fg_t = rows.tile([P, PAIR, PIXELS], BF16, name="fg_t")
-            nc.sync.dma_start(out=fg_t[:], in_=fg_rows[b, h, :, js, :])
-            bg_t = rows.tile([P, PAIR, PIXELS], BF16, name="bg_t")
-            nc.sync.dma_start(out=bg_t[:], in_=bg_rows[b, h, :, js, :])
-            return sim_t, fg_t, bg_t
+        def load_unit(k):
+            sim_t = rows.tile([P, TILES, PIXELS], BF16, name="sim_t")
+            fg_t = rows.tile([P, TILES, PIXELS], BF16, name="fg_t")
+            bg_t = rows.tile([P, TILES, PIXELS], BF16, name="bg_t")
+            nc.sync.dma_start(out=sim_t[:], in_=sim_rows[k, :, :, :])
+            nc.sync.dma_start(out=fg_t[:], in_=fg_rows[k, :, :, :])
+            nc.sync.dma_start(out=bg_t[:], in_=bg_rows[k, :, :, :])
+            row_tiles[k] = (sim_t, fg_t, bg_t)
 
-        def load_channels(b, x_t, first):
-            for t in range(first, first + QUAD, PAIR):
-                nc.sync.dma_start(out=x_t[:, t : t + PAIR, :], in_=x_rows[b, :, t : t + PAIR, :])
+        def load_channels(b, half):
+            if half == 0:
+                x_tiles[b] = image.tile([P, C_TILES, PIXELS], BF16, name="x_t")
+            ts = slice(half * C_TILES // 2, (half + 1) * C_TILES // 2)
+            nc.sync.dma_start(out=x_tiles[b][:, ts, :], in_=x_rows[b, :, ts, :])
 
-        def turn(source, grouped_words):
+        def turn_words(source, grouped_words):
             words = source.bitcast(F32)
             bank = turned.tile([P, PASSES, PLANES, P], F32, name="bank")
             for g in range(PASSES):
                 for u in range(PLANES):
-                    first = g * PLANES * P
+                    base = g * PLANES * P
                     nc.tensor.transpose(
-                        bank[:, g, u, :], words[:, first + u : first + PLANES * P : PLANES], identity[:]
+                        bank[:, g, u, :], words[:, base + u : base + PLANES * P : PLANES], identity[:]
                     )
             nc.scalar.copy(out=grouped_words, in_=bank[:].rearrange("k g u r -> k g r u"))
+
+        def on_vector(k, j):
+            return (TILES * k + j) % VECTOR_EVERY == VECTOR_EVERY - 1
+
+        def quantise_channels(b, c_pair):
+            if c_pair == 0:
+                x_codes = image.tile([P, C_TILES, PASSES, P], U32, name="x_codes", align_bytes=64)
+                x_scales = image.tile([P, C_TILES, PASSES, P], U8, name="x_scales", align_bytes=64)
+                x_packed[b] = (x_codes, x_scales)
+            x_codes, x_scales = x_packed[b]
+            x_grouped = packed.tile([P, PAIR, PASSES, P, PACK], BF16, name="x_grouped", align_bytes=64)
+            x_words = x_grouped[:].bitcast(F32)
+            first = PAIR * c_pair
+            for i in range(PAIR):
+                turn_words(x_tiles[b][:, first + i, :], x_words[:, i, :, :, :])
+            cs = slice(first, first + PAIR)
+            nc.vector.quantize_mx(
+                out=x_codes[:, cs, :, :].rearrange("k t g c -> k (t g c)").bitcast(FP8X4),
+                scales=x_scales[:, cs, :, :].rearrange("k t g c -> k (t g c)"),
+                in_=x_grouped[:].rearrange("k t g c v -> k (t g c v)"),
+            )
 
         def by_word(row):
             return row.rearrange("n (g k t) -> n g k t", k=P, t=PACK)
@@ -98,52 +116,63 @@ def tile_sgan_pb_kernel(tc, sim_fg, fg_sim, bg_sim, x, gamma, out):
         def into_blocks(blocks):
             return blocks.rearrange("n (g t) k -> n g k t", t=PACK)
 
-        def normalise_pair(tiles, q, a_grouped):
-            sim_t, fg_t, bg_t = tiles
-            lowest = stats.tile([P, PAIR], F32, name="lowest")
-            total = stats.tile([P, PAIR], F32, name="total")
-            divisor = stats.tile([P, PAIR], F32, name="divisor")
-            inverse = stats.tile([P, PAIR], F32, name="inverse")
-            for i in range(PAIR):
+        def mask_rows(k):
+            sim_t, fg_t, bg_t = row_tiles[k]
+            lowest = stats.tile([P, TILES], F32, name="lowest")
+            total = stats.tile([P, TILES], F32, name="total")
+            divisor = stats.tile([P, TILES], F32, name="divisor")
+            inverse = stats.tile([P, TILES], F32, name="inverse")
+            for j in range(TILES):
                 unread = work.tile([P, PIXELS], BF16, name="unread", bufs=2)
                 nc.vector.tensor_scalar(
                     out=unread[:],
-                    in0=sim_t[:, i, :],
+                    in0=sim_t[:, j, :],
                     scalar1=1.0,
                     scalar2=None,
                     op0=ALU.mult,
                     op1=ALU.min,
-                    accum_out=lowest[:, i : i + 1],
+                    accum_out=lowest[:, j : j + 1],
                 )
             masked = []
-            for i in range(PAIR):
+            for j in range(TILES):
                 x1 = work.tile([P, PIXELS], F32, name="x1")
                 nc.vector.scalar_tensor_tensor(
                     out=x1[:],
-                    in0=sim_t[:, i, :],
-                    scalar=lowest[:, i : i + 1],
-                    in1=fg_t[:, i, :],
+                    in0=sim_t[:, j, :],
+                    scalar=lowest[:, j : j + 1],
+                    in1=fg_t[:, j, :],
                     op0=ALU.subtract,
                     op1=ALU.mult,
-                    accum_out=total[:, i : i + 1],
+                    accum_out=total[:, j : j + 1],
                 )
                 masked.append(x1)
             nc.vector.tensor_scalar_add(out=divisor[:], in0=total[:], scalar1=EPS)
             nc.vector.reciprocal(out=inverse[:], in_=divisor[:])
-            for i in range(PAIR):
-                j = PAIR * q + i
-                bg_f32 = None
-                if j >= MATMUL_TILES:
-                    bg_f32 = work.tile([P, PASSES * PACK, P], F32, name="bg_f32", bufs=2)
-                    nc.scalar.copy(out=into_blocks(bg_f32[:]), in_=by_word(bg_t[:, i, :]))
-                scaled = work.tile([P, PASSES * PACK, P], F32, name="scaled")
+            return masked, inverse
+
+        def turn_rows(k, masked, inverse, a_grouped):
+            bg_t = row_tiles[k][2]
+            a_words = a_grouped[:].bitcast(F32)
+            for j in range(TILES):
+                if on_vector(k, j):
+                    a_rows = work.tile([P, PIXELS], BF16, name="a_rows", bufs=2)
+                    nc.vector.scalar_tensor_tensor(
+                        out=a_rows[:],
+                        in0=masked[j][:],
+                        scalar=inverse[:, j : j + 1],
+                        in1=bg_t[:, j, :],
+                        op0=ALU.mult,
+                        op1=ALU.add,
+                    )
+                    turn_words(a_rows[:], a_words[:, :, j * P : (j + 1) * P, :])
+                    continue
+                scaled = work.tile([P, PASSES * PACK, P], F32, name="scaled", bufs=3)
                 nc.scalar.activation(
                     out=into_blocks(scaled[:]),
-                    in_=by_word(masked[i][:]),
+                    in_=by_word(masked[j][:]),
                     func=ACT.Copy,
-                    scale=inverse[:, i : i + 1],
+                    scale=inverse[:, j : j + 1],
                 )
-                first = j * P
                 for g in range(PASSES):
                     bank = turned.tile([P, PACK, P], F32, name="bank")
                     for t in range(PACK):
@@ -156,40 +185,21 @@ def tile_sgan_pb_kernel(tc, sim_fg, fg_sim, bg_sim, x, gamma, out):
                             start=True,
                             stop=False,
                         )
-                        if bg_f32 is None:
-                            nc.tensor.matmul(
-                                out=bank[:, t, :],
-                                lhsT=bg_t[:, i, g * K_PASS + t : (g + 1) * K_PASS : PACK],
-                                rhs=identity_bf16[:],
-                                start=False,
-                                stop=True,
-                            )
-                        else:
-                            nc.tensor.matmul(
-                                out=bank[:, t, :],
-                                lhsT=bg_f32[:, block, :],
-                                rhs=identity[:],
-                                is_transpose=True,
-                                start=False,
-                                stop=True,
-                            )
+                        nc.tensor.matmul(
+                            out=bank[:, t, :],
+                            lhsT=bg_t[:, j, g * K_PASS + t : (g + 1) * K_PASS : PACK],
+                            rhs=identity_bf16[:],
+                            start=False,
+                            stop=True,
+                        )
                     nc.scalar.copy(
-                        out=a_grouped[:, g, first : first + P, :], in_=bank[:].rearrange("k t r -> k r t")
+                        out=a_grouped[:, g, j * P : (j + 1) * P, :], in_=bank[:].rearrange("k t r -> k r t")
                     )
 
-        def quantise_channels(x_t, x_codes, x_scales):
-            for first in range(0, C_TILES, QUAD):
-                x_grouped = packed.tile([P, QUAD, PASSES, P, PACK], BF16, name="x_grouped", align_bytes=64)
-                x_words = x_grouped[:].bitcast(F32)
-                for i in range(QUAD):
-                    turn(x_t[:, first + i, :], x_words[:, i, :, :, :])
-                nc.vector.quantize_mx(
-                    out=x_codes[:, first : first + QUAD, :, :].rearrange("k t g c -> k (t g c)").bitcast(FP8X4),
-                    scales=x_scales[:, first : first + QUAD, :, :].rearrange("k t g c -> k (t g c)"),
-                    in_=x_grouped[:].rearrange("k t g c v -> k (t g c v)"),
-                )
-
-        def multiply_unit(b, h, a_grouped, x_t, x_codes, x_scales):
+        def multiply_unit(k, a_grouped):
+            b, s = divmod(k, UNITS)
+            x_t = x_tiles[b]
+            x_codes, x_scales = x_packed[b]
             a_codes = packed.tile([P, PASSES, UNIT], U32, name="a_codes", align_bytes=64)
             a_scales = packed.tile([P, PASSES, UNIT], U8, name="a_scales", align_bytes=64)
             nc.vector.quantize_mx(
@@ -197,15 +207,22 @@ def tile_sgan_pb_kernel(tc, sim_fg, fg_sim, bg_sim, x, gamma, out):
                 scales=a_scales[:].rearrange("k g n -> k (g n)"),
                 in_=a_grouped[:].rearrange("k g n v -> k (g n v)"),
             )
-            pixels = slice(h * UNIT, h * UNIT + UNIT)
-            for first in range(0, C_TILES, PAIR):
-                result = work.tile([P, PAIR, UNIT], F32, name="result")
+            part = s % STORE_UNITS
+            if part == 0:
+                results[b, s // STORE_UNITS] = work.tile(
+                    [P, C_TILES, STORE_UNITS * UNIT], F32, name="result", bufs=2
+                )
+            result = results[b, s // STORE_UNITS]
+            pixels = slice(s * UNIT, (s + 1) * UNIT)
+            columns = slice(part * UNIT, (part + 1) * UNIT)
+            for c_pair in range(C_PAIRS):
+                cs = slice(PAIR * c_pair, PAIR * (c_pair + 1))
+                context = sums.tile([P, PAIR, UNIT], F32, name="context")
                 for i in range(PAIR):
-                    t = first + i
-                    context = sums.tile([P, UNIT], F32, name="context")
+                    t = PAIR * c_pair + i
                     for g in range(PASSES):
                         nc.tensor.matmul_mx(
-                            out=context[:],
+                            out=context[:, i, :],
                             lhsT=x_codes[:, t, g, :].bitcast(FP8X4),
                             lhsT_scale=x_scales[:, t, g, :],
                             rhs=a_codes[:, g, :].bitcast(FP8X4),
@@ -213,44 +230,50 @@ def tile_sgan_pb_kernel(tc, sim_fg, fg_sim, bg_sim, x, gamma, out):
                             start=(g == 0),
                             stop=(g == PASSES - 1),
                         )
-                    nc.vector.scalar_tensor_tensor(
-                        out=result[:, i, :].rearrange("c (p j) -> c p j", j=ROW_TILES),
-                        in0=context[:].rearrange("c (j p) -> c p j", j=ROW_TILES),
-                        scalar=gamma_f32[:, 0:1],
-                        in1=x_t[:, t, pixels].rearrange("c (p j) -> c p j", j=ROW_TILES),
-                        op0=ALU.mult,
-                        op1=ALU.add,
-                    )
-                nc.sync.dma_start(out=out_rows[b, :, first : first + PAIR, pixels], in_=result[:])
+                nc.vector.scalar_tensor_tensor(
+                    out=result[:, cs, columns],
+                    in0=context[:],
+                    scalar=gamma_f32[:, 0:1],
+                    in1=x_t[:, cs, pixels],
+                    op0=ALU.mult,
+                    op1=ALU.add,
+                )
+                last = k == BATCH * UNITS - 1
+                if last:
+                    nc.sync.dma_start(out=out_rows[b, :, cs, pixels], in_=result[:, cs, columns])
+            if k == BATCH * UNITS - 2:
+                nc.sync.dma_start(out=out_rows[b, :, :, pixels], in_=result[:, :, columns])
+            elif part == STORE_UNITS - 1 and not last:
+                whole = slice((s - part) * UNIT, (s + 1) * UNIT)
+                for half in range(2):
+                    ts = slice(half * C_TILES // 2, (half + 1) * C_TILES // 2)
+                    nc.sync.dma_start(out=out_rows[b, :, ts, whole], in_=result[:, ts, :])
 
-        loaded = {}
-        x_tiles = {}
+        load_unit(0)
+        nc.sync.dma_start(out=gamma_bf16[:], in_=gamma.partition_broadcast(P))
+        load_channels(0, 0)
+        load_unit(1)
+        load_channels(0, 1)
+        load_unit(2)
+        load_unit(3)
+        load_channels(1, 0)
+        load_channels(1, 1)
+        load_unit(4)
+        load_unit(5)
 
-        def issue_loads(k):
-            if k >= PAIRS:
-                return
-            b, h, q = place(k)
-            loaded[k] = load_pair(k)
-            if h == 0:
-                if q == 0:
-                    x_tiles[b] = image.tile([P, C_TILES, PIXELS], BF16, name="x_t")
-                load_channels(b, x_tiles[b], q * QUAD)
-
-        for k in range(AHEAD):
-            issue_loads(k)
-
-        x_packed = {}
-        a_grouped = None
-        for k in range(PAIRS):
-            b, h, q = place(k)
-            issue_loads(k + AHEAD)
-            if q == 0:
-                a_grouped = packed.tile([P, PASSES, UNIT, PACK], BF16, name="a_grouped", align_bytes=64)
-            normalise_pair(loaded[k], q, a_grouped)
-            if h == 0 and q == 0:
-                x_codes = image.tile([P, C_TILES, PASSES, P], U32, name="x_codes", align_bytes=64)
-                x_scales = image.tile([P, C_TILES, PASSES, P], U8, name="x_scales", align_bytes=64)
-                quantise_channels(x_tiles[b], x_codes, x_scales)
-                x_packed[b] = (x_codes, x_scales)
-            if q == ROW_TILES // PAIR - 1:
-                multiply_unit(b, h, a_grouped, x_tiles[b], x_packed[b][0], x_packed[b][1])
+        for k in range(BATCH * UNITS):
+            masked, inverse = mask_rows(k)
+            if k == 0:
+                nc.vector.tensor_copy(out=gamma_f32[:], in_=gamma_bf16[:])
+            a_grouped = packed.tile([P, PASSES, UNIT, PACK], BF16, name="a_grouped", align_bytes=64)
+            turn_rows(k, masked, inverse, a_grouped)
+            if k == 0:
+                for c_pair in range(C_PAIRS):
+                    quantise_channels(0, c_pair)
+            elif k <= C_PAIRS - 1:
+                quantise_channels(1, k - 1)
+            if k == C_PAIRS - 1:
+                quantise_channels(1, k)
+            multiply_unit(k, a_grouped)
+            if 6 + k < BATCH * UNITS:
+                load_unit(6 + k)

@@ -10,6 +10,7 @@ U8 = mybir.dt.uint8
 FP8X4 = mybir.dt.float8_e4m3fn_x4
 ALU = mybir.AluOpType
 ACT = mybir.ActivationFunctionType
+ENGINE = mybir.EngineType
 
 P = 128
 BATCH = 2
@@ -22,12 +23,14 @@ PASSES = PIXELS // K_PASS
 PLANES = 2
 TILES = 2
 UNIT = TILES * P
-UNITS = PIXELS // UNIT
+IMAGE_UNITS = PIXELS // UNIT
+UNITS = BATCH * IMAGE_UNITS
 STORE_UNITS = 2
 C_TILES = CHANNELS // P
 PAIR = 2
 C_PAIRS = C_TILES // PAIR
-VECTOR_EVERY = 4
+ROW_BUFS = 6
+LEAD = 2
 
 FLOPS = 2 * BATCH * PIXELS * PIXELS * CHANNELS
 
@@ -35,17 +38,17 @@ FLOPS = 2 * BATCH * PIXELS * PIXELS * CHANNELS
 def tile_sgan_pb_kernel(tc, sim_fg, fg_sim, bg_sim, x, gamma, out):
     nc = tc.nc
 
-    sim_rows = sim_fg.rearrange("b (s j p) m -> (b s) p j m", s=UNITS, j=TILES)
-    fg_rows = fg_sim.rearrange("b (s j p) m -> (b s) p j m", s=UNITS, j=TILES)
-    bg_rows = bg_sim.rearrange("b (s j p) m -> (b s) p j m", s=UNITS, j=TILES)
+    sim_rows = sim_fg.rearrange("b (s j p) m -> (b s) p j m", s=IMAGE_UNITS, j=TILES)
+    fg_rows = fg_sim.rearrange("b (s j p) m -> (b s) p j m", s=IMAGE_UNITS, j=TILES)
+    bg_rows = bg_sim.rearrange("b (s j p) m -> (b s) p j m", s=IMAGE_UNITS, j=TILES)
     x_rows = x.rearrange("b (p t) r s -> b p t (r s)", t=C_TILES)
     out_rows = out.rearrange("b (p t) r s -> b p t (r s)", t=C_TILES)
 
     with ExitStack() as ctx:
         const = ctx.enter_context(tc.tile_pool(name="const", bufs=1))
-        rows = ctx.enter_context(tc.tile_pool(name="rows", bufs=6))
+        rows = ctx.enter_context(tc.tile_pool(name="rows", bufs=ROW_BUFS))
         image = ctx.enter_context(tc.tile_pool(name="image", bufs=BATCH))
-        work = ctx.enter_context(tc.tile_pool(name="work", bufs=4))
+        work = ctx.enter_context(tc.tile_pool(name="work", bufs=2))
         stats = ctx.enter_context(tc.tile_pool(name="stats", bufs=4))
         packed = ctx.enter_context(tc.tile_pool(name="packed", bufs=2))
         turned = ctx.enter_context(tc.psum_pool(name="turned", bufs=4))
@@ -58,25 +61,79 @@ def tile_sgan_pb_kernel(tc, sim_fg, fg_sim, bg_sim, x, gamma, out):
         gamma_bf16 = const.tile([P, 1], BF16, name="gamma_bf16")
         gamma_f32 = const.tile([P, 1], F32, name="gamma_f32")
 
-        row_tiles = {}
-        x_tiles = {}
+        sim_tiles, fg_tiles, bg_tiles, x_tiles = {}, {}, {}, {}
+        statistics = {}
+        masked = {}
+        a_grouped = {}
+        a_packed = {}
+        x_grouped = {}
         x_packed = {}
+        contexts = {}
         results = {}
 
-        def load_unit(k):
-            sim_t = rows.tile([P, TILES, PIXELS], BF16, name="sim_t")
-            fg_t = rows.tile([P, TILES, PIXELS], BF16, name="fg_t")
-            bg_t = rows.tile([P, TILES, PIXELS], BF16, name="bg_t")
-            nc.sync.dma_start(out=sim_t[:], in_=sim_rows[k, :, :, :])
-            nc.sync.dma_start(out=fg_t[:], in_=fg_rows[k, :, :, :])
-            nc.sync.dma_start(out=bg_t[:], in_=bg_rows[k, :, :, :])
-            row_tiles[k] = (sim_t, fg_t, bg_t)
+        def load_rows(k, tiles, source, name):
+            tiles[k] = rows.tile([P, TILES, PIXELS], BF16, name=name)
+            nc.sync.dma_start(out=tiles[k][:], in_=source[k, :, :, :])
+
+        def load_sim(k):
+            load_rows(k, sim_tiles, sim_rows, "sim_t")
+
+        def load_fg(k):
+            load_rows(k, fg_tiles, fg_rows, "fg_t")
+
+        def load_bg(k):
+            load_rows(k, bg_tiles, bg_rows, "bg_t")
 
         def load_channels(b, half):
             if half == 0:
                 x_tiles[b] = image.tile([P, C_TILES, PIXELS], BF16, name="x_t")
             ts = slice(half * C_TILES // 2, (half + 1) * C_TILES // 2)
             nc.sync.dma_start(out=x_tiles[b][:, ts, :], in_=x_rows[b, :, ts, :])
+
+        def by_word(row):
+            return row.rearrange("n (g k t) -> n g k t", k=P, t=PACK)
+
+        def into_blocks(blocks):
+            return blocks.rearrange("n (g t) k -> n g k t", t=PACK)
+
+        def minimum(k, j):
+            if j == 0:
+                statistics[k] = [
+                    stats.tile([P, TILES], F32, name=name) for name in ("lowest", "total", "divisor", "inverse")
+                ]
+            unread = work.tile([P, PIXELS], BF16, name="unread")
+            nc.vector.tensor_scalar(
+                out=unread[:],
+                in0=sim_tiles[k][:, j, :],
+                scalar1=1.0,
+                scalar2=None,
+                op0=ALU.mult,
+                op1=ALU.min,
+                accum_out=statistics[k][0][:, j : j + 1],
+            )
+
+        def mask(k, j):
+            lowest, total = statistics[k][0], statistics[k][1]
+            x1 = work.tile([P, PIXELS], F32, name="x1", bufs=4)
+            nc.vector.scalar_tensor_tensor(
+                out=x1[:],
+                in0=sim_tiles[k][:, j, :],
+                scalar=lowest[:, j : j + 1],
+                in1=fg_tiles[k][:, j, :],
+                op0=ALU.subtract,
+                op1=ALU.mult,
+                accum_out=total[:, j : j + 1],
+            )
+            masked[k, j] = x1
+
+        def divisor(k):
+            nc.vector.tensor_scalar_add(out=statistics[k][2][:], in0=statistics[k][1][:], scalar1=EPS)
+
+        def invert(k):
+            nc.vector.reciprocal(out=statistics[k][3][:], in_=statistics[k][2][:])
+            a_grouped[k] = packed.tile(
+                [P, PASSES, UNIT, PACK], BF16, name="a_grouped", align_bytes=64, bufs=LEAD + 1
+            )
 
         def turn_words(source, grouped_words):
             words = source.bitcast(F32)
@@ -89,8 +146,13 @@ def tile_sgan_pb_kernel(tc, sim_fg, fg_sim, bg_sim, x, gamma, out):
                     )
             nc.scalar.copy(out=grouped_words, in_=bank[:].rearrange("k g u r -> k g r u"))
 
-        def on_vector(k, j):
-            return (TILES * k + j) % VECTOR_EVERY == VECTOR_EVERY - 1
+        def turn_channels(b, c_pair):
+            x_grouped[b, c_pair] = packed.tile(
+                [P, PAIR, PASSES, P, PACK], BF16, name="x_grouped", align_bytes=64, bufs=3
+            )
+            x_words = x_grouped[b, c_pair][:].bitcast(F32)
+            for i in range(PAIR):
+                turn_words(x_tiles[b][:, PAIR * c_pair + i, :], x_words[:, i, :, :, :])
 
         def quantise_channels(b, c_pair):
             if c_pair == 0:
@@ -98,125 +160,77 @@ def tile_sgan_pb_kernel(tc, sim_fg, fg_sim, bg_sim, x, gamma, out):
                 x_scales = image.tile([P, C_TILES, PASSES, P], U8, name="x_scales", align_bytes=64)
                 x_packed[b] = (x_codes, x_scales)
             x_codes, x_scales = x_packed[b]
-            x_grouped = packed.tile([P, PAIR, PASSES, P, PACK], BF16, name="x_grouped", align_bytes=64)
-            x_words = x_grouped[:].bitcast(F32)
-            first = PAIR * c_pair
-            for i in range(PAIR):
-                turn_words(x_tiles[b][:, first + i, :], x_words[:, i, :, :, :])
-            cs = slice(first, first + PAIR)
+            cs = slice(PAIR * c_pair, PAIR * (c_pair + 1))
             nc.vector.quantize_mx(
                 out=x_codes[:, cs, :, :].rearrange("k t g c -> k (t g c)").bitcast(FP8X4),
                 scales=x_scales[:, cs, :, :].rearrange("k t g c -> k (t g c)"),
-                in_=x_grouped[:].rearrange("k t g c v -> k (t g c v)"),
+                in_=x_grouped[b, c_pair][:].rearrange("k t g c v -> k (t g c v)"),
             )
 
-        def by_word(row):
-            return row.rearrange("n (g k t) -> n g k t", k=P, t=PACK)
+        def scale(k, j):
+            scaled = work.tile([P, PASSES * PACK, P], F32, name="scaled", bufs=3)
+            nc.scalar.activation(
+                out=into_blocks(scaled[:]),
+                in_=by_word(masked[k, j][:]),
+                func=ACT.Copy,
+                scale=statistics[k][3][:, j : j + 1],
+            )
+            return scaled
 
-        def into_blocks(blocks):
-            return blocks.rearrange("n (g t) k -> n g k t", t=PACK)
-
-        def mask_rows(k):
-            sim_t, fg_t, bg_t = row_tiles[k]
-            lowest = stats.tile([P, TILES], F32, name="lowest")
-            total = stats.tile([P, TILES], F32, name="total")
-            divisor = stats.tile([P, TILES], F32, name="divisor")
-            inverse = stats.tile([P, TILES], F32, name="inverse")
-            for j in range(TILES):
-                unread = work.tile([P, PIXELS], BF16, name="unread", bufs=2)
-                nc.vector.tensor_scalar(
-                    out=unread[:],
-                    in0=sim_t[:, j, :],
-                    scalar1=1.0,
-                    scalar2=None,
-                    op0=ALU.mult,
-                    op1=ALU.min,
-                    accum_out=lowest[:, j : j + 1],
-                )
-            masked = []
-            for j in range(TILES):
-                x1 = work.tile([P, PIXELS], F32, name="x1")
-                nc.vector.scalar_tensor_tensor(
-                    out=x1[:],
-                    in0=sim_t[:, j, :],
-                    scalar=lowest[:, j : j + 1],
-                    in1=fg_t[:, j, :],
-                    op0=ALU.subtract,
-                    op1=ALU.mult,
-                    accum_out=total[:, j : j + 1],
-                )
-                masked.append(x1)
-            nc.vector.tensor_scalar_add(out=divisor[:], in0=total[:], scalar1=EPS)
-            nc.vector.reciprocal(out=inverse[:], in_=divisor[:])
-            return masked, inverse
-
-        def turn_rows(k, masked, inverse, a_grouped):
-            bg_t = row_tiles[k][2]
-            a_words = a_grouped[:].bitcast(F32)
-            for j in range(TILES):
-                if on_vector(k, j):
-                    a_rows = work.tile([P, PIXELS], BF16, name="a_rows", bufs=2)
-                    nc.vector.scalar_tensor_tensor(
-                        out=a_rows[:],
-                        in0=masked[j][:],
-                        scalar=inverse[:, j : j + 1],
-                        in1=bg_t[:, j, :],
-                        op0=ALU.mult,
-                        op1=ALU.add,
+        def turn_sum(k, j, scaled):
+            for g in range(PASSES):
+                bank = turned.tile([P, PACK, P], F32, name="bank")
+                for t in range(PACK):
+                    block = g * PACK + t
+                    nc.tensor.matmul(
+                        out=bank[:, t, :],
+                        lhsT=scaled[:, block, :],
+                        rhs=identity[:],
+                        is_transpose=True,
+                        start=True,
+                        stop=False,
                     )
-                    turn_words(a_rows[:], a_words[:, :, j * P : (j + 1) * P, :])
-                    continue
-                scaled = work.tile([P, PASSES * PACK, P], F32, name="scaled", bufs=3)
-                nc.scalar.activation(
-                    out=into_blocks(scaled[:]),
-                    in_=by_word(masked[j][:]),
-                    func=ACT.Copy,
-                    scale=inverse[:, j : j + 1],
-                )
-                for g in range(PASSES):
-                    bank = turned.tile([P, PACK, P], F32, name="bank")
-                    for t in range(PACK):
-                        block = g * PACK + t
-                        nc.tensor.matmul(
-                            out=bank[:, t, :],
-                            lhsT=scaled[:, block, :],
-                            rhs=identity[:],
-                            is_transpose=True,
-                            start=True,
-                            stop=False,
-                        )
-                        nc.tensor.matmul(
-                            out=bank[:, t, :],
-                            lhsT=bg_t[:, j, g * K_PASS + t : (g + 1) * K_PASS : PACK],
-                            rhs=identity_bf16[:],
-                            start=False,
-                            stop=True,
-                        )
-                    nc.scalar.copy(
-                        out=a_grouped[:, g, j * P : (j + 1) * P, :], in_=bank[:].rearrange("k t r -> k r t")
+                    nc.tensor.matmul(
+                        out=bank[:, t, :],
+                        lhsT=bg_tiles[k][:, j, g * K_PASS + t : (g + 1) * K_PASS : PACK],
+                        rhs=identity_bf16[:],
+                        start=False,
+                        stop=True,
                     )
+                nc.scalar.copy(
+                    out=a_grouped[k][:, g, j * P : (j + 1) * P, :], in_=bank[:].rearrange("k t r -> k r t")
+                )
 
-        def multiply_unit(k, a_grouped):
-            b, s = divmod(k, UNITS)
-            x_t = x_tiles[b]
-            x_codes, x_scales = x_packed[b]
+        def add_on_vector(k, j):
+            a_rows = work.tile([P, PIXELS], BF16, name="a_rows")
+            nc.vector.scalar_tensor_tensor(
+                out=a_rows[:],
+                in0=masked[k, j][:],
+                scalar=statistics[k][3][:, j : j + 1],
+                in1=bg_tiles[k][:, j, :],
+                op0=ALU.mult,
+                op1=ALU.add,
+            )
+            return a_rows
+
+        def turn_rows(k, j, a_rows):
+            a_words = a_grouped[k][:].bitcast(F32)
+            turn_words(a_rows[:], a_words[:, :, j * P : (j + 1) * P, :])
+
+        def quantise_rows(k):
             a_codes = packed.tile([P, PASSES, UNIT], U32, name="a_codes", align_bytes=64)
             a_scales = packed.tile([P, PASSES, UNIT], U8, name="a_scales", align_bytes=64)
             nc.vector.quantize_mx(
                 out=a_codes[:].rearrange("k g n -> k (g n)").bitcast(FP8X4),
                 scales=a_scales[:].rearrange("k g n -> k (g n)"),
-                in_=a_grouped[:].rearrange("k g n v -> k (g n v)"),
+                in_=a_grouped[k][:].rearrange("k g n v -> k (g n v)"),
             )
-            part = s % STORE_UNITS
-            if part == 0:
-                results[b, s // STORE_UNITS] = work.tile(
-                    [P, C_TILES, STORE_UNITS * UNIT], F32, name="result", bufs=2
-                )
-            result = results[b, s // STORE_UNITS]
-            pixels = slice(s * UNIT, (s + 1) * UNIT)
-            columns = slice(part * UNIT, (part + 1) * UNIT)
+            a_packed[k] = (a_codes, a_scales)
+
+        def multiply(k):
+            x_codes, x_scales = x_packed[k // IMAGE_UNITS]
+            a_codes, a_scales = a_packed[k]
             for c_pair in range(C_PAIRS):
-                cs = slice(PAIR * c_pair, PAIR * (c_pair + 1))
                 context = sums.tile([P, PAIR, UNIT], F32, name="context")
                 for i in range(PAIR):
                     t = PAIR * c_pair + i
@@ -230,50 +244,102 @@ def tile_sgan_pb_kernel(tc, sim_fg, fg_sim, bg_sim, x, gamma, out):
                             start=(g == 0),
                             stop=(g == PASSES - 1),
                         )
-                nc.vector.scalar_tensor_tensor(
-                    out=result[:, cs, columns],
-                    in0=context[:],
-                    scalar=gamma_f32[:, 0:1],
-                    in1=x_t[:, cs, pixels],
-                    op0=ALU.mult,
-                    op1=ALU.add,
-                )
-                last = k == BATCH * UNITS - 1
-                if last:
-                    nc.sync.dma_start(out=out_rows[b, :, cs, pixels], in_=result[:, cs, columns])
-            if k == BATCH * UNITS - 2:
-                nc.sync.dma_start(out=out_rows[b, :, :, pixels], in_=result[:, :, columns])
-            elif part == STORE_UNITS - 1 and not last:
-                whole = slice((s - part) * UNIT, (s + 1) * UNIT)
-                for half in range(2):
-                    ts = slice(half * C_TILES // 2, (half + 1) * C_TILES // 2)
-                    nc.sync.dma_start(out=out_rows[b, :, ts, whole], in_=result[:, ts, :])
+                contexts[k, c_pair] = context
 
-        load_unit(0)
+        def finish(k, c_pair):
+            b, s = divmod(k, IMAGE_UNITS)
+            group, part = divmod(s, STORE_UNITS)
+            if part == 0 and c_pair == 0:
+                results[b, group] = work.tile([P, C_TILES, STORE_UNITS * UNIT], F32, name="result")
+            result = results[b, group]
+            cs = slice(PAIR * c_pair, PAIR * (c_pair + 1))
+            pixels = slice(s * UNIT, (s + 1) * UNIT)
+            columns = slice(part * UNIT, (part + 1) * UNIT)
+            nc.vector.scalar_tensor_tensor(
+                out=result[:, cs, columns],
+                in0=contexts[k, c_pair][:],
+                scalar=gamma_f32[:, 0:1],
+                in1=x_tiles[b][:, cs, pixels],
+                op0=ALU.mult,
+                op1=ALU.add,
+            )
+            if k == UNITS - 1:
+                nc.sync.dma_start(out=out_rows[b, :, cs, pixels], in_=result[:, cs, columns])
+            elif k == UNITS - 2:
+                if c_pair == C_PAIRS - 1:
+                    nc.sync.dma_start(out=out_rows[b, :, :, pixels], in_=result[:, :, columns])
+            elif part == STORE_UNITS - 1 and c_pair % 2 == 1:
+                ts = slice(PAIR * (c_pair - 1), PAIR * (c_pair + 1))
+                whole = slice(group * STORE_UNITS * UNIT, (group + 1) * STORE_UNITS * UNIT)
+                nc.sync.dma_start(out=out_rows[b, :, ts, whole], in_=result[:, ts, :])
+
+        load_sim(0)
+        load_fg(0)
         nc.sync.dma_start(out=gamma_bf16[:], in_=gamma.partition_broadcast(P))
+        load_sim(1)
+        load_bg(0)
         load_channels(0, 0)
-        load_unit(1)
+        load_fg(1)
         load_channels(0, 1)
-        load_unit(2)
-        load_unit(3)
+        load_sim(2)
+        load_fg(2)
+        load_bg(1)
+        load_sim(3)
+        load_fg(3)
+        load_bg(2)
         load_channels(1, 0)
         load_channels(1, 1)
-        load_unit(4)
-        load_unit(5)
+        load_bg(3)
+        for k in range(4, ROW_BUFS):
+            load_sim(k)
+            load_fg(k)
+            load_bg(k)
 
-        for k in range(BATCH * UNITS):
-            masked, inverse = mask_rows(k)
-            if k == 0:
-                nc.vector.tensor_copy(out=gamma_f32[:], in_=gamma_bf16[:])
-            a_grouped = packed.tile([P, PASSES, UNIT, PACK], BF16, name="a_grouped", align_bytes=64)
-            turn_rows(k, masked, inverse, a_grouped)
-            if k == 0:
-                for c_pair in range(C_PAIRS):
-                    quantise_channels(0, c_pair)
-            elif k <= C_PAIRS - 1:
-                quantise_channels(1, k - 1)
-            if k == C_PAIRS - 1:
-                quantise_channels(1, k)
-            multiply_unit(k, a_grouped)
-            if 6 + k < BATCH * UNITS:
-                load_unit(6 + k)
+        channel_pairs = {0: [(0, 0), (0, 1)], 1: [(0, 2), (0, 3)]}
+        channel_pairs.update({3: [(1, 0)], 4: [(1, 1)], 5: [(1, 2), (1, 3)]})
+
+        with tc.manual_schedule(engines={ENGINE.PE, ENGINE.DVE, ENGINE.Activation}):
+            for j in range(TILES):
+                minimum(0, j)
+            nc.vector.tensor_copy(out=gamma_f32[:], in_=gamma_bf16[:])
+            for k in range(UNITS + LEAD):
+                late = k - LEAD
+                if late >= 0 and k < UNITS:
+                    quantise_rows(late)
+                if k < UNITS:
+                    mask(k, 0)
+                for b, c_pair in channel_pairs.get(k, []):
+                    turn_channels(b, c_pair)
+                for b, c_pair in channel_pairs.get(k - 1, []):
+                    quantise_channels(b, c_pair)
+                if late >= 0 and k >= UNITS:
+                    quantise_rows(late)
+                if late >= 0:
+                    multiply(late)
+                if k < UNITS:
+                    mask(k, 1)
+                if k + 1 < UNITS:
+                    minimum(k + 1, 0)
+                if k < UNITS:
+                    divisor(k)
+                if k + 1 < UNITS:
+                    minimum(k + 1, 1)
+                if k < UNITS:
+                    invert(k)
+                if late >= 0:
+                    finish(late, 0)
+                    finish(late, 1)
+                if k in (0, UNITS - 1):
+                    for j in range(TILES):
+                        turn_rows(k, j, add_on_vector(k, j))
+                elif k < UNITS:
+                    scaled = [scale(k, j) for j in range(TILES)]
+                    for j in range(TILES):
+                        turn_sum(k, j, scaled[j])
+                if late >= 0:
+                    finish(late, 2)
+                    finish(late, 3)
+                if ROW_BUFS + k < UNITS:
+                    load_sim(ROW_BUFS + k)
+                    load_fg(ROW_BUFS + k)
+                    load_bg(ROW_BUFS + k)

@@ -178,27 +178,28 @@ def tile_sgan_pb_kernel(tc, sim_fg, fg_sim, bg_sim, x, gamma, out):
             return scaled
 
         def turn_sum(k, j, scaled):
-            for g in range(PASSES):
-                bank = turned.tile([P, PACK, P], F32, name="bank")
-                for t in range(PACK):
-                    block = g * PACK + t
+            banks = [turned.tile([P, PACK, P], F32, name="bank") for g in range(PASSES)]
+            for t in range(PACK):
+                for g in range(PASSES):
                     nc.tensor.matmul(
-                        out=bank[:, t, :],
-                        lhsT=scaled[:, block, :],
-                        rhs=identity[:],
-                        is_transpose=True,
+                        out=banks[g][:, t, :],
+                        lhsT=bg_tiles[k][:, j, g * K_PASS + t : (g + 1) * K_PASS : PACK],
+                        rhs=identity_bf16[:],
                         start=True,
                         stop=False,
                     )
+                for g in range(PASSES):
                     nc.tensor.matmul(
-                        out=bank[:, t, :],
-                        lhsT=bg_tiles[k][:, j, g * K_PASS + t : (g + 1) * K_PASS : PACK],
-                        rhs=identity_bf16[:],
+                        out=banks[g][:, t, :],
+                        lhsT=scaled[:, g * PACK + t, :],
+                        rhs=identity[:],
+                        is_transpose=True,
                         start=False,
                         stop=True,
                     )
+            for g in range(PASSES):
                 nc.scalar.copy(
-                    out=a_grouped[k][:, g, j * P : (j + 1) * P, :], in_=bank[:].rearrange("k t r -> k r t")
+                    out=a_grouped[k][:, g, j * P : (j + 1) * P, :], in_=banks[g][:].rearrange("k t r -> k r t")
                 )
 
         def add_on_vector(k, j):

@@ -25,12 +25,13 @@ TILES = 2
 UNIT = TILES * P
 IMAGE_UNITS = PIXELS // UNIT
 UNITS = BATCH * IMAGE_UNITS
-STORE_UNITS = 2
 C_TILES = CHANNELS // P
 PAIR = 2
 C_PAIRS = C_TILES // PAIR
 ROW_BUFS = 6
-LEAD = 2
+LAG = 3
+VECTOR_UNITS = (0, UNITS - 1)
+CAST_TILE = 1
 
 FLOPS = 2 * BATCH * PIXELS * PIXELS * CHANNELS
 
@@ -64,6 +65,15 @@ def tile_sgan_pb_kernel(tc, sim_fg, fg_sim, bg_sim, x, gamma, out):
         sim_tiles, fg_tiles, bg_tiles, x_tiles = {}, {}, {}, {}
         statistics = {}
         masked = {}
+        scaled = {}
+        bg_blocks = {}
+        pending = {}
+
+        def empty(key):
+            for target, source in pending.pop(key):
+                nc.scalar.copy(out=target, in_=source)
+
+        added = {}
         a_grouped = {}
         a_packed = {}
         x_grouped = {}
@@ -73,7 +83,11 @@ def tile_sgan_pb_kernel(tc, sim_fg, fg_sim, bg_sim, x, gamma, out):
 
         def load_rows(k, tiles, source, name):
             tiles[k] = rows.tile([P, TILES, PIXELS], BF16, name=name)
-            nc.sync.dma_start(out=tiles[k][:], in_=source[k, :, :, :])
+            if k > 0:
+                nc.sync.dma_start(out=tiles[k][:], in_=source[k, :, :, :])
+            else:
+                for j in range(TILES):
+                    nc.sync.dma_start(out=tiles[k][:, j, :], in_=source[k, :, j, :])
 
         def load_sim(k):
             load_rows(k, sim_tiles, sim_rows, "sim_t")
@@ -132,7 +146,7 @@ def tile_sgan_pb_kernel(tc, sim_fg, fg_sim, bg_sim, x, gamma, out):
         def invert(k):
             nc.vector.reciprocal(out=statistics[k][3][:], in_=statistics[k][2][:])
             a_grouped[k] = packed.tile(
-                [P, PASSES, UNIT, PACK], BF16, name="a_grouped", align_bytes=64, bufs=LEAD + 1
+                [P, PASSES, UNIT, PACK], BF16, name="a_grouped", align_bytes=64, bufs=LAG
             )
 
         def turn_words(source, grouped_words):
@@ -144,15 +158,16 @@ def tile_sgan_pb_kernel(tc, sim_fg, fg_sim, bg_sim, x, gamma, out):
                     nc.tensor.transpose(
                         bank[:, g, u, :], words[:, base + u : base + PLANES * P : PLANES], identity[:]
                     )
-            nc.scalar.copy(out=grouped_words, in_=bank[:].rearrange("k g u r -> k g r u"))
+            return [(grouped_words, bank[:].rearrange("k g u r -> k g r u"))]
 
-        def turn_channels(b, c_pair):
-            x_grouped[b, c_pair] = packed.tile(
-                [P, PAIR, PASSES, P, PACK], BF16, name="x_grouped", align_bytes=64, bufs=3
-            )
+        def turn_channel(b, t):
+            c_pair, i = divmod(t, PAIR)
+            if i == 0:
+                x_grouped[b, c_pair] = packed.tile(
+                    [P, PAIR, PASSES, P, PACK], BF16, name="x_grouped", align_bytes=64, bufs=3
+                )
             x_words = x_grouped[b, c_pair][:].bitcast(F32)
-            for i in range(PAIR):
-                turn_words(x_tiles[b][:, PAIR * c_pair + i, :], x_words[:, i, :, :, :])
+            pending["x", b, t] = turn_words(x_tiles[b][:, t, :], x_words[:, i, :, :, :])
 
         def quantise_channels(b, c_pair):
             if c_pair == 0:
@@ -168,39 +183,54 @@ def tile_sgan_pb_kernel(tc, sim_fg, fg_sim, bg_sim, x, gamma, out):
             )
 
         def scale(k, j):
-            scaled = work.tile([P, PASSES * PACK, P], F32, name="scaled", bufs=3)
+            blocks = work.tile([P, PASSES * PACK, P], F32, name="blocks", bufs=3)
             nc.scalar.activation(
-                out=into_blocks(scaled[:]),
+                out=into_blocks(blocks[:]),
                 in_=by_word(masked[k, j][:]),
                 func=ACT.Copy,
                 scale=statistics[k][3][:, j : j + 1],
             )
-            return scaled
+            scaled[k, j] = blocks
 
-        def turn_sum(k, j, scaled):
+        def cast(k, j):
+            blocks = work.tile([P, PASSES * PACK, P], F32, name="bg_f32")
+            nc.scalar.copy(out=into_blocks(blocks[:]), in_=by_word(bg_tiles[k][:, j, :]))
+            bg_blocks[k, j] = blocks
+
+        def turn_sum(k, j):
             banks = [turned.tile([P, PACK, P], F32, name="bank") for g in range(PASSES)]
             for t in range(PACK):
                 for g in range(PASSES):
-                    nc.tensor.matmul(
-                        out=banks[g][:, t, :],
-                        lhsT=bg_tiles[k][:, j, g * K_PASS + t : (g + 1) * K_PASS : PACK],
-                        rhs=identity_bf16[:],
-                        start=True,
-                        stop=False,
-                    )
+                    if (k, j) in bg_blocks:
+                        nc.tensor.matmul(
+                            out=banks[g][:, t, :],
+                            lhsT=bg_blocks[k, j][:, g * PACK + t, :],
+                            rhs=identity[:],
+                            is_transpose=True,
+                            start=True,
+                            stop=False,
+                        )
+                    else:
+                        nc.tensor.matmul(
+                            out=banks[g][:, t, :],
+                            lhsT=bg_tiles[k][:, j, g * K_PASS + t : (g + 1) * K_PASS : PACK],
+                            rhs=identity_bf16[:],
+                            start=True,
+                            stop=False,
+                        )
                 for g in range(PASSES):
                     nc.tensor.matmul(
                         out=banks[g][:, t, :],
-                        lhsT=scaled[:, g * PACK + t, :],
+                        lhsT=scaled[k, j][:, g * PACK + t, :],
                         rhs=identity[:],
                         is_transpose=True,
                         start=False,
                         stop=True,
                     )
-            for g in range(PASSES):
-                nc.scalar.copy(
-                    out=a_grouped[k][:, g, j * P : (j + 1) * P, :], in_=banks[g][:].rearrange("k t r -> k r t")
-                )
+            pending["a", k, j] = [
+                (a_grouped[k][:, g, j * P : (j + 1) * P, :], banks[g][:].rearrange("k t r -> k r t"))
+                for g in range(PASSES)
+            ]
 
         def add_on_vector(k, j):
             a_rows = work.tile([P, PIXELS], BF16, name="a_rows")
@@ -212,11 +242,11 @@ def tile_sgan_pb_kernel(tc, sim_fg, fg_sim, bg_sim, x, gamma, out):
                 op0=ALU.mult,
                 op1=ALU.add,
             )
-            return a_rows
+            added[k, j] = a_rows
 
-        def turn_rows(k, j, a_rows):
+        def turn_rows(k, j):
             a_words = a_grouped[k][:].bitcast(F32)
-            turn_words(a_rows[:], a_words[:, :, j * P : (j + 1) * P, :])
+            pending["a", k, j] = turn_words(added[k, j][:], a_words[:, :, j * P : (j + 1) * P, :])
 
         def quantise_rows(k):
             a_codes = packed.tile([P, PASSES, UNIT], U32, name="a_codes", align_bytes=64)
@@ -228,36 +258,33 @@ def tile_sgan_pb_kernel(tc, sim_fg, fg_sim, bg_sim, x, gamma, out):
             )
             a_packed[k] = (a_codes, a_scales)
 
-        def multiply(k):
+        def multiply(k, c_pair):
             x_codes, x_scales = x_packed[k // IMAGE_UNITS]
             a_codes, a_scales = a_packed[k]
-            for c_pair in range(C_PAIRS):
-                context = sums.tile([P, PAIR, UNIT], F32, name="context")
-                for i in range(PAIR):
-                    t = PAIR * c_pair + i
-                    for g in range(PASSES):
-                        nc.tensor.matmul_mx(
-                            out=context[:, i, :],
-                            lhsT=x_codes[:, t, g, :].bitcast(FP8X4),
-                            lhsT_scale=x_scales[:, t, g, :],
-                            rhs=a_codes[:, g, :].bitcast(FP8X4),
-                            rhs_scale=a_scales[:, g, :],
-                            start=(g == 0),
-                            stop=(g == PASSES - 1),
-                        )
-                contexts[k, c_pair] = context
+            context = sums.tile([P, PAIR, UNIT], F32, name="context")
+            for i in range(PAIR):
+                t = PAIR * c_pair + i
+                for g in range(PASSES):
+                    nc.tensor.matmul_mx(
+                        out=context[:, i, :],
+                        lhsT=x_codes[:, t, g, :].bitcast(FP8X4),
+                        lhsT_scale=x_scales[:, t, g, :],
+                        rhs=a_codes[:, g, :].bitcast(FP8X4),
+                        rhs_scale=a_scales[:, g, :],
+                        start=(g == 0),
+                        stop=(g == PASSES - 1),
+                    )
+            contexts[k, c_pair] = context
 
         def finish(k, c_pair):
             b, s = divmod(k, IMAGE_UNITS)
-            group, part = divmod(s, STORE_UNITS)
-            if part == 0 and c_pair == 0:
-                results[b, group] = work.tile([P, C_TILES, STORE_UNITS * UNIT], F32, name="result")
-            result = results[b, group]
+            if c_pair == 0:
+                results[k] = work.tile([P, C_TILES, UNIT], F32, name="result", bufs=3)
+            result = results[k]
             cs = slice(PAIR * c_pair, PAIR * (c_pair + 1))
             pixels = slice(s * UNIT, (s + 1) * UNIT)
-            columns = slice(part * UNIT, (part + 1) * UNIT)
             nc.vector.scalar_tensor_tensor(
-                out=result[:, cs, columns],
+                out=result[:, cs, :],
                 in0=contexts[k, c_pair][:],
                 scalar=gamma_f32[:, 0:1],
                 in1=x_tiles[b][:, cs, pixels],
@@ -265,18 +292,18 @@ def tile_sgan_pb_kernel(tc, sim_fg, fg_sim, bg_sim, x, gamma, out):
                 op1=ALU.add,
             )
             if k == UNITS - 1:
-                nc.sync.dma_start(out=out_rows[b, :, cs, pixels], in_=result[:, cs, columns])
-            elif k == UNITS - 2:
-                if c_pair == C_PAIRS - 1:
-                    nc.sync.dma_start(out=out_rows[b, :, :, pixels], in_=result[:, :, columns])
-            elif part == STORE_UNITS - 1 and c_pair % 2 == 1:
+                nc.sync.dma_start(out=out_rows[b, :, cs, pixels], in_=result[:, cs, :])
+            elif c_pair % 2 == 1:
                 ts = slice(PAIR * (c_pair - 1), PAIR * (c_pair + 1))
-                whole = slice(group * STORE_UNITS * UNIT, (group + 1) * STORE_UNITS * UNIT)
-                nc.sync.dma_start(out=out_rows[b, :, ts, whole], in_=result[:, ts, :])
+                nc.sync.dma_start(out=out_rows[b, :, ts, pixels], in_=result[:, ts, :])
+
+        def load_unit(k):
+            load_sim(k)
+            load_fg(k)
+            load_bg(k)
 
         load_sim(0)
         load_fg(0)
-        nc.sync.dma_start(out=gamma_bf16[:], in_=gamma.partition_broadcast(P))
         load_sim(1)
         load_bg(0)
         load_channels(0, 0)
@@ -285,6 +312,7 @@ def tile_sgan_pb_kernel(tc, sim_fg, fg_sim, bg_sim, x, gamma, out):
         load_sim(2)
         load_fg(2)
         load_bg(1)
+        nc.sync.dma_start(out=gamma_bf16[:], in_=gamma.partition_broadcast(P))
         load_sim(3)
         load_fg(3)
         load_bg(2)
@@ -292,55 +320,76 @@ def tile_sgan_pb_kernel(tc, sim_fg, fg_sim, bg_sim, x, gamma, out):
         load_channels(1, 1)
         load_bg(3)
         for k in range(4, ROW_BUFS):
-            load_sim(k)
-            load_fg(k)
-            load_bg(k)
+            load_unit(k)
 
-        channel_pairs = {0: [(0, 0), (0, 1)], 1: [(0, 2), (0, 3)]}
-        channel_pairs.update({3: [(1, 0)], 4: [(1, 1)], 5: [(1, 2), (1, 3)]})
+        turn_steps = {
+            0: [(0, t) for t in range(0, 4)],
+            1: [(0, t) for t in range(4, 8)],
+            3: [(1, 0), (1, 1)],
+            4: [(1, 2), (1, 3)],
+            5: [(1, t) for t in range(4, 8)],
+        }
+        quantise_steps = {1: [(0, 0), (0, 1)], 2: [(0, 2), (0, 3)], 4: [(1, 0)], 5: [(1, 1)], 6: [(1, 2), (1, 3)]}
 
         with tc.manual_schedule(engines={ENGINE.PE, ENGINE.DVE, ENGINE.Activation}):
             for j in range(TILES):
                 minimum(0, j)
-            nc.vector.tensor_copy(out=gamma_f32[:], in_=gamma_bf16[:])
-            for k in range(UNITS + LEAD):
-                late = k - LEAD
-                if late >= 0 and k < UNITS:
-                    quantise_rows(late)
-                if k < UNITS:
-                    mask(k, 0)
-                for b, c_pair in channel_pairs.get(k, []):
-                    turn_channels(b, c_pair)
-                for b, c_pair in channel_pairs.get(k - 1, []):
-                    quantise_channels(b, c_pair)
-                if late >= 0 and k >= UNITS:
-                    quantise_rows(late)
-                if late >= 0:
-                    multiply(late)
-                if k < UNITS:
-                    mask(k, 1)
-                if k + 1 < UNITS:
-                    minimum(k + 1, 0)
-                if k < UNITS:
-                    divisor(k)
-                if k + 1 < UNITS:
-                    minimum(k + 1, 1)
-                if k < UNITS:
-                    invert(k)
-                if late >= 0:
+            for k in range(UNITS + LAG):
+                fresh = k if k < UNITS else None
+                turning = k - 1 if 1 <= k <= UNITS else None
+                packed_now = k - 2 if 2 <= k < UNITS + 2 else None
+                late = k - LAG if k >= LAG else None
+                if fresh is not None:
+                    mask(fresh, 0)
+                if late is not None:
+                    for c_pair in range(C_PAIRS):
+                        multiply(late, c_pair)
+                if fresh is not None:
+                    mask(fresh, 1)
+                if turning is not None:
+                    if turning in VECTOR_UNITS:
+                        for j in range(TILES):
+                            turn_rows(turning, j)
+                            empty(("a", turning, j))
+                    else:
+                        for j in range(TILES):
+                            scale(turning, j)
+                        if fresh is not None and fresh not in VECTOR_UNITS:
+                            cast(fresh, CAST_TILE)
+                        for j in range(TILES):
+                            turn_sum(turning, j)
+                            empty(("a", turning, j))
+                for b, t in turn_steps.get(k, []):
+                    turn_channel(b, t)
+                for b, t in turn_steps.get(k, []):
+                    empty(("x", b, t))
+                if late is not None:
                     finish(late, 0)
+                    if fresh is not None:
+                        divisor(fresh)
+                    elif packed_now is not None:
+                        quantise_rows(packed_now)
                     finish(late, 1)
-                if k in (0, UNITS - 1):
-                    for j in range(TILES):
-                        turn_rows(k, j, add_on_vector(k, j))
-                elif k < UNITS:
-                    scaled = [scale(k, j) for j in range(TILES)]
-                    for j in range(TILES):
-                        turn_sum(k, j, scaled[j])
-                if late >= 0:
+                    if fresh is not None:
+                        invert(fresh)
                     finish(late, 2)
                     finish(late, 3)
-                if ROW_BUFS + k < UNITS:
-                    load_sim(ROW_BUFS + k)
-                    load_fg(ROW_BUFS + k)
-                    load_bg(ROW_BUFS + k)
+                if fresh is not None and packed_now is not None:
+                    quantise_rows(packed_now)
+                for b, c_pair in quantise_steps.get(k, []):
+                    quantise_channels(b, c_pair)
+                if k + 1 < UNITS:
+                    minimum(k + 1, 0)
+                if late is None:
+                    divisor(fresh)
+                if k + 1 < UNITS:
+                    minimum(k + 1, 1)
+                if late is None:
+                    invert(fresh)
+                if fresh in VECTOR_UNITS:
+                    for j in range(TILES):
+                        add_on_vector(fresh, j)
+                if k == LAG - 1:
+                    nc.vector.tensor_copy(out=gamma_f32[:], in_=gamma_bf16[:])
+                if k > 0 and k - 1 + ROW_BUFS < UNITS:
+                    load_unit(k - 1 + ROW_BUFS)

@@ -27,8 +27,10 @@ IMAGE_UNITS = PIXELS // UNIT
 UNITS = BATCH * IMAGE_UNITS
 C_TILES = CHANNELS // P
 PAIR = 2
+QUAD = 4
 C_PAIRS = C_TILES // PAIR
 ROW_BUFS = 6
+STORE_UNITS = 2
 LAG = 3
 VECTOR_UNITS = (0, UNITS - 1)
 CAST_TILE = 1
@@ -60,7 +62,6 @@ def tile_sgan_pb_kernel(tc, sim_fg, fg_sim, bg_sim, x, gamma, out):
         identity_bf16 = const.tile([P, P], BF16, name="identity_bf16")
         make_identity(nc, identity_bf16[:])
         gamma_bf16 = const.tile([P, 1], BF16, name="gamma_bf16")
-        gamma_f32 = const.tile([P, 1], F32, name="gamma_f32")
 
         sim_tiles, fg_tiles, bg_tiles, x_tiles = {}, {}, {}, {}
         statistics = {}
@@ -141,7 +142,7 @@ def tile_sgan_pb_kernel(tc, sim_fg, fg_sim, bg_sim, x, gamma, out):
             masked[k, j] = x1
 
         def divisor(k):
-            nc.vector.tensor_scalar_add(out=statistics[k][2][:], in0=statistics[k][1][:], scalar1=EPS)
+            nc.gpsimd.tensor_scalar_add(out=statistics[k][2][:], in0=statistics[k][1][:], scalar1=EPS)
 
         def invert(k):
             nc.vector.reciprocal(out=statistics[k][3][:], in_=statistics[k][2][:])
@@ -161,25 +162,23 @@ def tile_sgan_pb_kernel(tc, sim_fg, fg_sim, bg_sim, x, gamma, out):
             return [(grouped_words, bank[:].rearrange("k g u r -> k g r u"))]
 
         def turn_channel(b, t):
-            c_pair, i = divmod(t, PAIR)
+            quad, i = divmod(t, QUAD)
             if i == 0:
-                x_grouped[b, c_pair] = packed.tile(
-                    [P, PAIR, PASSES, P, PACK], BF16, name="x_grouped", align_bytes=64, bufs=3
-                )
-            x_words = x_grouped[b, c_pair][:].bitcast(F32)
+                x_grouped[b, quad] = packed.tile([P, QUAD, PASSES, P, PACK], BF16, name="x_grouped", align_bytes=64)
+            x_words = x_grouped[b, quad][:].bitcast(F32)
             pending["x", b, t] = turn_words(x_tiles[b][:, t, :], x_words[:, i, :, :, :])
 
-        def quantise_channels(b, c_pair):
-            if c_pair == 0:
+        def quantise_channels(b, quad):
+            if quad == 0:
                 x_codes = image.tile([P, C_TILES, PASSES, P], U32, name="x_codes", align_bytes=64)
                 x_scales = image.tile([P, C_TILES, PASSES, P], U8, name="x_scales", align_bytes=64)
                 x_packed[b] = (x_codes, x_scales)
             x_codes, x_scales = x_packed[b]
-            cs = slice(PAIR * c_pair, PAIR * (c_pair + 1))
+            cs = slice(QUAD * quad, QUAD * (quad + 1))
             nc.vector.quantize_mx(
                 out=x_codes[:, cs, :, :].rearrange("k t g c -> k (t g c)").bitcast(FP8X4),
                 scales=x_scales[:, cs, :, :].rearrange("k t g c -> k (t g c)"),
-                in_=x_grouped[b, c_pair][:].rearrange("k t g c v -> k (t g c v)"),
+                in_=x_grouped[b, quad][:].rearrange("k t g c v -> k (t g c v)"),
             )
 
         def scale(k, j):
@@ -278,24 +277,31 @@ def tile_sgan_pb_kernel(tc, sim_fg, fg_sim, bg_sim, x, gamma, out):
 
         def finish(k, c_pair):
             b, s = divmod(k, IMAGE_UNITS)
-            if c_pair == 0:
-                results[k] = work.tile([P, C_TILES, UNIT], F32, name="result", bufs=3)
+            part = k % STORE_UNITS
+            if c_pair == 0 and part == 0:
+                result = work.tile([P, C_TILES, STORE_UNITS * UNIT], F32, name="result")
+                results.update({k + i: result for i in range(STORE_UNITS)})
             result = results[k]
             cs = slice(PAIR * c_pair, PAIR * (c_pair + 1))
             pixels = slice(s * UNIT, (s + 1) * UNIT)
+            columns = slice(part * UNIT, (part + 1) * UNIT)
             nc.vector.scalar_tensor_tensor(
-                out=result[:, cs, :],
+                out=result[:, cs, columns],
                 in0=contexts[k, c_pair][:],
-                scalar=gamma_f32[:, 0:1],
+                scalar=gamma_bf16[:, 0:1],
                 in1=x_tiles[b][:, cs, pixels],
                 op0=ALU.mult,
                 op1=ALU.add,
             )
             if k == UNITS - 1:
-                nc.sync.dma_start(out=out_rows[b, :, cs, pixels], in_=result[:, cs, :])
+                nc.sync.dma_start(out=out_rows[b, :, cs, pixels], in_=result[:, cs, columns])
             elif c_pair % 2 == 1:
                 ts = slice(PAIR * (c_pair - 1), PAIR * (c_pair + 1))
-                nc.sync.dma_start(out=out_rows[b, :, ts, pixels], in_=result[:, ts, :])
+                if k >= IMAGE_UNITS:
+                    nc.sync.dma_start(out=out_rows[b, :, ts, pixels], in_=result[:, ts, columns])
+                elif part == STORE_UNITS - 1:
+                    pixels = slice((s + 1 - STORE_UNITS) * UNIT, (s + 1) * UNIT)
+                    nc.sync.dma_start(out=out_rows[b, :, ts, pixels], in_=result[:, ts, :])
 
         def load_unit(k):
             load_sim(k)
@@ -329,7 +335,7 @@ def tile_sgan_pb_kernel(tc, sim_fg, fg_sim, bg_sim, x, gamma, out):
             4: [(1, 2), (1, 3)],
             5: [(1, t) for t in range(4, 8)],
         }
-        quantise_steps = {1: [(0, 0), (0, 1)], 2: [(0, 2), (0, 3)], 4: [(1, 0)], 5: [(1, 1)], 6: [(1, 2), (1, 3)]}
+        quantise_steps = {1: [(0, 0)], 2: [(0, 1)], 5: [(1, 0)], 6: [(1, 1)]}
 
         with tc.manual_schedule(engines={ENGINE.PE, ENGINE.DVE, ENGINE.Activation}):
             for j in range(TILES):
@@ -376,8 +382,8 @@ def tile_sgan_pb_kernel(tc, sim_fg, fg_sim, bg_sim, x, gamma, out):
                     finish(late, 3)
                 if fresh is not None and packed_now is not None:
                     quantise_rows(packed_now)
-                for b, c_pair in quantise_steps.get(k, []):
-                    quantise_channels(b, c_pair)
+                for b, quad in quantise_steps.get(k, []):
+                    quantise_channels(b, quad)
                 if k + 1 < UNITS:
                     minimum(k + 1, 0)
                 if late is None:
@@ -389,7 +395,5 @@ def tile_sgan_pb_kernel(tc, sim_fg, fg_sim, bg_sim, x, gamma, out):
                 if fresh in VECTOR_UNITS:
                     for j in range(TILES):
                         add_on_vector(fresh, j)
-                if k == LAG - 1:
-                    nc.vector.tensor_copy(out=gamma_f32[:], in_=gamma_bf16[:])
                 if k > 0 and k - 1 + ROW_BUFS < UNITS:
                     load_unit(k - 1 + ROW_BUFS)

@@ -360,8 +360,6 @@ def tile_sgan_pb_kernel(tc, sim_fg, fg_sim, bg_sim, x, gamma, out):
                     else:
                         for j in range(TILES):
                             scale(turning, j)
-                        if fresh is not None and fresh not in VECTOR_UNITS:
-                            cast(fresh, CAST_TILE)
                         for j in range(TILES):
                             turn_sum(turning, j)
                             empty(("a", turning, j))

@@ -33,7 +33,6 @@ ROW_BUFS = 6
 STORE_UNITS = 2
 LAG = 3
 VECTOR_UNITS = (0, UNITS - 1)
-CAST_TILE = 1
 
 FLOPS = 2 * BATCH * PIXELS * PIXELS * CHANNELS
 
@@ -67,7 +66,6 @@ def tile_sgan_pb_kernel(tc, sim_fg, fg_sim, bg_sim, x, gamma, out):
         statistics = {}
         masked = {}
         scaled = {}
-        bg_blocks = {}
         pending = {}
 
         def empty(key):
@@ -191,40 +189,26 @@ def tile_sgan_pb_kernel(tc, sim_fg, fg_sim, bg_sim, x, gamma, out):
             )
             scaled[k, j] = blocks
 
-        def cast(k, j):
-            blocks = work.tile([P, PASSES * PACK, P], F32, name="bg_f32")
-            nc.scalar.copy(out=into_blocks(blocks[:]), in_=by_word(bg_tiles[k][:, j, :]))
-            bg_blocks[k, j] = blocks
-
         def turn_sum(k, j):
             banks = [turned.tile([P, PACK, P], F32, name="bank") for g in range(PASSES)]
-            for t in range(PACK):
-                for g in range(PASSES):
-                    if (k, j) in bg_blocks:
-                        nc.tensor.matmul(
-                            out=banks[g][:, t, :],
-                            lhsT=bg_blocks[k, j][:, g * PACK + t, :],
-                            rhs=identity[:],
-                            is_transpose=True,
-                            start=True,
-                            stop=False,
-                        )
-                    else:
-                        nc.tensor.matmul(
-                            out=banks[g][:, t, :],
-                            lhsT=bg_tiles[k][:, j, g * K_PASS + t : (g + 1) * K_PASS : PACK],
-                            rhs=identity_bf16[:],
-                            start=True,
-                            stop=False,
-                        )
-                for g in range(PASSES):
+            for g in range(PASSES):
+                for t in range(PACK):
+                    nc.tensor.matmul(
+                        out=banks[g][:, t, :],
+                        lhsT=bg_tiles[k][:, j, g * K_PASS + t : (g + 1) * K_PASS : PACK],
+                        rhs=identity_bf16[:],
+                        start=(t == 0),
+                        stop=False,
+                    )
+            for g in range(PASSES):
+                for t in range(PACK):
                     nc.tensor.matmul(
                         out=banks[g][:, t, :],
                         lhsT=scaled[k, j][:, g * PACK + t, :],
                         rhs=identity[:],
                         is_transpose=True,
                         start=False,
-                        stop=True,
+                        stop=(t == PACK - 1),
                     )
             pending["a", k, j] = [
                 (a_grouped[k][:, g, j * P : (j + 1) * P, :], banks[g][:].rearrange("k t r -> k r t"))

@@ -32,6 +32,7 @@ C_PAIRS = C_TILES // PAIR
 ROW_BUFS = 6
 STORE_UNITS = 2
 LAG = 3
+GPSIMD_PAIR = 0
 VECTOR_UNITS = (0, UNITS - 1)
 
 FLOPS = 2 * BATCH * PIXELS * PIXELS * CHANNELS
@@ -61,6 +62,7 @@ def tile_sgan_pb_kernel(tc, sim_fg, fg_sim, bg_sim, x, gamma, out):
         identity_bf16 = const.tile([P, P], BF16, name="identity_bf16")
         make_identity(nc, identity_bf16[:])
         gamma_bf16 = const.tile([P, 1], BF16, name="gamma_bf16")
+        gamma_f32 = const.tile([P, 1], F32, name="gamma_f32")
 
         sim_tiles, fg_tiles, bg_tiles, x_tiles = {}, {}, {}, {}
         statistics = {}
@@ -79,6 +81,7 @@ def tile_sgan_pb_kernel(tc, sim_fg, fg_sim, bg_sim, x, gamma, out):
         x_packed = {}
         contexts = {}
         results = {}
+        gated = {}
 
         def load_rows(k, tiles, source, name):
             tiles[k] = rows.tile([P, TILES, PIXELS], BF16, name=name)
@@ -140,7 +143,7 @@ def tile_sgan_pb_kernel(tc, sim_fg, fg_sim, bg_sim, x, gamma, out):
             masked[k, j] = x1
 
         def divisor(k):
-            nc.gpsimd.tensor_scalar_add(out=statistics[k][2][:], in0=statistics[k][1][:], scalar1=EPS)
+            nc.scalar.activation(out=statistics[k][2][:], in_=statistics[k][1][:], func=ACT.Copy, bias=EPS)
 
         def invert(k):
             nc.vector.reciprocal(out=statistics[k][3][:], in_=statistics[k][2][:])
@@ -259,6 +262,12 @@ def tile_sgan_pb_kernel(tc, sim_fg, fg_sim, bg_sim, x, gamma, out):
                     )
             contexts[k, c_pair] = context
 
+        def gate(k, c_pair):
+            gated[k] = work.tile([P, PAIR, UNIT], F32, name="gated")
+            nc.scalar.activation(
+                out=gated[k][:], in_=contexts[k, c_pair][:], func=ACT.Copy, scale=gamma_f32[:, 0:1]
+            )
+
         def finish(k, c_pair):
             b, s = divmod(k, IMAGE_UNITS)
             part = k % STORE_UNITS
@@ -269,23 +278,33 @@ def tile_sgan_pb_kernel(tc, sim_fg, fg_sim, bg_sim, x, gamma, out):
             cs = slice(PAIR * c_pair, PAIR * (c_pair + 1))
             pixels = slice(s * UNIT, (s + 1) * UNIT)
             columns = slice(part * UNIT, (part + 1) * UNIT)
-            nc.vector.scalar_tensor_tensor(
-                out=result[:, cs, columns],
-                in0=contexts[k, c_pair][:],
-                scalar=gamma_bf16[:, 0:1],
-                in1=x_tiles[b][:, cs, pixels],
-                op0=ALU.mult,
-                op1=ALU.add,
-            )
-            if k == UNITS - 1:
-                nc.sync.dma_start(out=out_rows[b, :, cs, pixels], in_=result[:, cs, columns])
-            elif c_pair % 2 == 1:
-                ts = slice(PAIR * (c_pair - 1), PAIR * (c_pair + 1))
-                if k >= IMAGE_UNITS:
-                    nc.sync.dma_start(out=out_rows[b, :, ts, pixels], in_=result[:, ts, columns])
-                elif part == STORE_UNITS - 1:
-                    pixels = slice((s + 1 - STORE_UNITS) * UNIT, (s + 1) * UNIT)
-                    nc.sync.dma_start(out=out_rows[b, :, ts, pixels], in_=result[:, ts, :])
+            if c_pair == GPSIMD_PAIR:
+                nc.gpsimd.tensor_tensor(
+                    out=result[:, cs, columns], in0=gated[k][:], in1=x_tiles[b][:, cs, pixels], op=ALU.add
+                )
+            else:
+                nc.vector.scalar_tensor_tensor(
+                    out=result[:, cs, columns],
+                    in0=contexts[k, c_pair][:],
+                    scalar=gamma_bf16[:, 0:1],
+                    in1=x_tiles[b][:, cs, pixels],
+                    op0=ALU.mult,
+                    op1=ALU.add,
+                )
+
+        def store(k, first, pairs):
+            b, s = divmod(k, IMAGE_UNITS)
+            part = k % STORE_UNITS
+            ts = slice(PAIR * first, PAIR * (first + pairs))
+            if b == BATCH - 1:
+                columns = slice(part * UNIT, (part + 1) * UNIT)
+                pixels = slice(s * UNIT, (s + 1) * UNIT)
+            elif part == STORE_UNITS - 1:
+                columns = slice(0, STORE_UNITS * UNIT)
+                pixels = slice((s + 1 - STORE_UNITS) * UNIT, (s + 1) * UNIT)
+            else:
+                return
+            nc.sync.dma_start(out=out_rows[b, :, ts, pixels], in_=results[k][:, ts, columns])
 
         def load_unit(k):
             load_sim(k)
@@ -303,6 +322,7 @@ def tile_sgan_pb_kernel(tc, sim_fg, fg_sim, bg_sim, x, gamma, out):
         load_fg(2)
         load_bg(1)
         nc.sync.dma_start(out=gamma_bf16[:], in_=gamma.partition_broadcast(P))
+        nc.gpsimd.tensor_copy(out=gamma_f32[:], in_=gamma_bf16[:])
         load_sim(3)
         load_fg(3)
         load_bg(2)
@@ -336,40 +356,54 @@ def tile_sgan_pb_kernel(tc, sim_fg, fg_sim, bg_sim, x, gamma, out):
                         multiply(late, c_pair)
                 if fresh is not None:
                     mask(fresh, 1)
-                if turning is not None:
-                    if turning in VECTOR_UNITS:
-                        for j in range(TILES):
-                            turn_rows(turning, j)
-                            empty(("a", turning, j))
-                    else:
-                        for j in range(TILES):
-                            scale(turning, j)
-                        for j in range(TILES):
-                            turn_sum(turning, j)
-                            empty(("a", turning, j))
+                if late is not None and turning in (None, *VECTOR_UNITS):
+                    gate(late, GPSIMD_PAIR)
+                if turning in VECTOR_UNITS:
+                    for j in range(TILES):
+                        turn_rows(turning, j)
+                        empty(("a", turning, j))
+                elif turning is not None:
+                    for j in range(TILES):
+                        scale(turning, j)
+                    if late is not None:
+                        gate(late, GPSIMD_PAIR)
+                if fresh is not None:
+                    divisor(fresh)
+                if turning is not None and turning not in VECTOR_UNITS:
+                    for j in range(TILES):
+                        turn_sum(turning, j)
+                        empty(("a", turning, j))
                 for b, t in turn_steps.get(k, []):
                     turn_channel(b, t)
                 for b, t in turn_steps.get(k, []):
                     empty(("x", b, t))
                 if late is not None:
+                    last = late == UNITS - 1
                     finish(late, 0)
-                    if fresh is not None:
-                        divisor(fresh)
-                    elif packed_now is not None:
+                    if fresh is None and packed_now is not None:
                         quantise_rows(packed_now)
                     finish(late, 1)
+                    if last:
+                        store(late, 1, 1)
+                    else:
+                        store(late, 0, 2)
+                    finish(late, 2)
+                    if last:
+                        store(late, 2, 1)
+                        store(late, 0, 1)
                     if fresh is not None:
                         invert(fresh)
-                    finish(late, 2)
                     finish(late, 3)
+                    if last:
+                        store(late, 3, 1)
+                    else:
+                        store(late, 2, 2)
                 if fresh is not None and packed_now is not None:
                     quantise_rows(packed_now)
                 for b, quad in quantise_steps.get(k, []):
                     quantise_channels(b, quad)
                 if k + 1 < UNITS:
                     minimum(k + 1, 0)
-                if late is None:
-                    divisor(fresh)
                 if k + 1 < UNITS:
                     minimum(k + 1, 1)
                 if late is None:

@@ -143,7 +143,7 @@ def tile_sgan_pb_kernel(tc, sim_fg, fg_sim, bg_sim, x, gamma, out):
             masked[k, j] = x1
 
         def divisor(k):
-            nc.scalar.activation(out=statistics[k][2][:], in_=statistics[k][1][:], func=ACT.Copy, bias=EPS)
+            nc.gpsimd.tensor_scalar_add(out=statistics[k][2][:], in0=statistics[k][1][:], scalar1=EPS)
 
         def invert(k):
             nc.vector.reciprocal(out=statistics[k][3][:], in_=statistics[k][2][:])
@@ -341,7 +341,7 @@ def tile_sgan_pb_kernel(tc, sim_fg, fg_sim, bg_sim, x, gamma, out):
         }
         quantise_steps = {1: [(0, 0)], 2: [(0, 1)], 5: [(1, 0)], 6: [(1, 1)]}
 
-        with tc.manual_schedule(engines={ENGINE.PE, ENGINE.DVE, ENGINE.Activation}):
+        with tc.manual_schedule(engines={ENGINE.PE, ENGINE.DVE, ENGINE.Activation, ENGINE.Pool}):
             for j in range(TILES):
                 minimum(0, j)
             for k in range(UNITS + LAG):

@@ -327,10 +327,14 @@ def tile_sgan_pb_kernel(tc, sim_fg, fg_sim, bg_sim, x, gamma, out):
         load_fg(3)
         load_bg(2)
         load_channels(1, 0)
+        load_sim(4)
+        load_fg(4)
         load_channels(1, 1)
         load_bg(3)
-        for k in range(4, ROW_BUFS):
-            load_unit(k)
+        load_bg(4)
+        load_sim(5)
+        load_fg(5)
+        load_bg(5)
 
         turn_steps = {
             0: [(0, t) for t in range(0, 4)],

@@ -32,7 +32,6 @@ C_PAIRS = C_TILES // PAIR
 ROW_BUFS = 6
 STORE_UNITS = 2
 LAG = 3
-GPSIMD_PAIR = 0
 VECTOR_UNITS = (0, UNITS - 1)
 
 FLOPS = 2 * BATCH * PIXELS * PIXELS * CHANNELS
@@ -262,11 +261,13 @@ def tile_sgan_pb_kernel(tc, sim_fg, fg_sim, bg_sim, x, gamma, out):
                     )
             contexts[k, c_pair] = context
 
+        def gpsimd_pairs(k):
+            return (0,) if k <= IMAGE_UNITS + 1 else ()
+
         def gate(k, c_pair):
-            gated[k] = work.tile([P, PAIR, UNIT], F32, name="gated")
-            nc.scalar.activation(
-                out=gated[k][:], in_=contexts[k, c_pair][:], func=ACT.Copy, scale=gamma_f32[:, 0:1]
-            )
+            part = work.tile([P, PAIR, UNIT], F32, name="gated", bufs=3)
+            nc.scalar.activation(out=part[:], in_=contexts[k, c_pair][:], func=ACT.Copy, scale=gamma_f32[:, 0:1])
+            gated[k, c_pair] = part
 
         def finish(k, c_pair):
             b, s = divmod(k, IMAGE_UNITS)
@@ -278,9 +279,9 @@ def tile_sgan_pb_kernel(tc, sim_fg, fg_sim, bg_sim, x, gamma, out):
             cs = slice(PAIR * c_pair, PAIR * (c_pair + 1))
             pixels = slice(s * UNIT, (s + 1) * UNIT)
             columns = slice(part * UNIT, (part + 1) * UNIT)
-            if c_pair == GPSIMD_PAIR:
+            if (k, c_pair) in gated:
                 nc.gpsimd.tensor_tensor(
-                    out=result[:, cs, columns], in0=gated[k][:], in1=x_tiles[b][:, cs, pixels], op=ALU.add
+                    out=result[:, cs, columns], in0=gated[k, c_pair][:], in1=x_tiles[b][:, cs, pixels], op=ALU.add
                 )
             else:
                 nc.vector.scalar_tensor_tensor(
@@ -322,7 +323,6 @@ def tile_sgan_pb_kernel(tc, sim_fg, fg_sim, bg_sim, x, gamma, out):
         load_fg(2)
         load_bg(1)
         nc.sync.dma_start(out=gamma_bf16[:], in_=gamma.partition_broadcast(P))
-        nc.gpsimd.tensor_copy(out=gamma_f32[:], in_=gamma_bf16[:])
         load_sim(3)
         load_fg(3)
         load_bg(2)
@@ -348,20 +348,21 @@ def tile_sgan_pb_kernel(tc, sim_fg, fg_sim, bg_sim, x, gamma, out):
         with tc.manual_schedule(engines={ENGINE.PE, ENGINE.DVE, ENGINE.Activation, ENGINE.Pool}):
             for j in range(TILES):
                 minimum(0, j)
-            for k in range(UNITS + LAG):
+            for k in range(UNITS + LAG - 1):
                 fresh = k if k < UNITS else None
                 turning = k - 1 if 1 <= k <= UNITS else None
-                packed_now = k - 2 if 2 <= k < UNITS + 2 else None
-                late = k - LAG if k >= LAG else None
-                if fresh is not None:
-                    mask(fresh, 0)
+                packed_now = k - 2 if 2 <= k < UNITS else None
+                late = k - LAG if LAG <= k < UNITS else None
+                drained = k - LAG + 1 if k >= UNITS - 1 else None
+                draining = drained is not None
                 if late is not None:
                     for c_pair in range(C_PAIRS):
                         multiply(late, c_pair)
                 if fresh is not None:
+                    mask(fresh, 0)
+                    if draining:
+                        quantise_rows(packed_now)
                     mask(fresh, 1)
-                if late is not None and turning in (None, *VECTOR_UNITS):
-                    gate(late, GPSIMD_PAIR)
                 if turning in VECTOR_UNITS:
                     for j in range(TILES):
                         turn_rows(turning, j)
@@ -370,7 +371,10 @@ def tile_sgan_pb_kernel(tc, sim_fg, fg_sim, bg_sim, x, gamma, out):
                     for j in range(TILES):
                         scale(turning, j)
                     if late is not None:
-                        gate(late, GPSIMD_PAIR)
+                        for c_pair in gpsimd_pairs(late):
+                            gate(late, c_pair)
+                if k == LAG - 1:
+                    nc.scalar.copy(out=gamma_f32[:], in_=gamma_bf16[:])
                 if fresh is not None:
                     divisor(fresh)
                 if turning is not None and turning not in VECTOR_UNITS:
@@ -382,38 +386,38 @@ def tile_sgan_pb_kernel(tc, sim_fg, fg_sim, bg_sim, x, gamma, out):
                 for b, t in turn_steps.get(k, []):
                     empty(("x", b, t))
                 if late is not None:
-                    last = late == UNITS - 1
                     finish(late, 0)
-                    if fresh is None and packed_now is not None:
-                        quantise_rows(packed_now)
                     finish(late, 1)
-                    if last:
-                        store(late, 1, 1)
-                    else:
-                        store(late, 0, 2)
+                    store(late, 0, 2)
                     finish(late, 2)
-                    if last:
-                        store(late, 2, 1)
-                        store(late, 0, 1)
-                    if fresh is not None:
-                        invert(fresh)
+                    invert(fresh)
                     finish(late, 3)
-                    if last:
-                        store(late, 3, 1)
-                    else:
-                        store(late, 2, 2)
-                if fresh is not None and packed_now is not None:
+                    store(late, 2, 2)
+                if packed_now is not None and not draining:
                     quantise_rows(packed_now)
                 for b, quad in quantise_steps.get(k, []):
                     quantise_channels(b, quad)
                 if k + 1 < UNITS:
-                    minimum(k + 1, 0)
-                if k + 1 < UNITS:
-                    minimum(k + 1, 1)
-                if late is None:
+                    for j in range(TILES):
+                        minimum(k + 1, j)
+                if fresh is not None and late is None:
                     invert(fresh)
                 if fresh in VECTOR_UNITS:
                     for j in range(TILES):
                         add_on_vector(fresh, j)
+                if draining:
+                    last = drained == UNITS - 1
+                    for c_pair in range(C_PAIRS):
+                        multiply(drained, c_pair)
+                    for c_pair in gpsimd_pairs(drained):
+                        gate(drained, c_pair)
+                    for c_pair in range(C_PAIRS):
+                        finish(drained, c_pair)
+                        if last:
+                            store(drained, c_pair, 1)
+                        elif c_pair % 2 == 1:
+                            store(drained, c_pair - 1, 2)
+                        if c_pair == 1 and not last:
+                            quantise_rows(drained + 1)
                 if k > 0 and k - 1 + ROW_BUFS < UNITS:
                     load_unit(k - 1 + ROW_BUFS)

from contextlib import ExitStack

import concourse.mybir as mybir
from concourse.masks import make_identity

F32 = mybir.dt.float32
BF16 = mybir.dt.bfloat16
U32 = mybir.dt.uint32
U8 = mybir.dt.uint8
FP8X4 = mybir.dt.float8_e4m3fn_x4
ALU = mybir.AluOpType
ACT = mybir.ActivationFunctionType
ENGINE = mybir.EngineType

P = 128
BATCH = 2
PIXELS = 1024
CHANNELS = 1024
EPS = 1e-5
PACK = 4
K_PASS = P * PACK
PASSES = PIXELS // K_PASS
PLANES = 2
TILES = 2
UNIT = TILES * P
IMAGE_UNITS = PIXELS // UNIT
UNITS = BATCH * IMAGE_UNITS
C_TILES = CHANNELS // P
PAIR = 2
QUAD = 4
C_PAIRS = C_TILES // PAIR
ROW_BUFS = 6
STORE_UNITS = 2
LAG = 3
VECTOR_UNITS = (0, UNITS - 1)

FLOPS = 2 * BATCH * PIXELS * PIXELS * CHANNELS


def tile_sgan_pb_kernel(tc, sim_fg, fg_sim, bg_sim, x, gamma, out):
    nc = tc.nc

    sim_rows = sim_fg.rearrange("b (s j p) m -> (b s) p j m", s=IMAGE_UNITS, j=TILES)
    fg_rows = fg_sim.rearrange("b (s j p) m -> (b s) p j m", s=IMAGE_UNITS, j=TILES)
    bg_rows = bg_sim.rearrange("b (s j p) m -> (b s) p j m", s=IMAGE_UNITS, j=TILES)
    x_rows = x.rearrange("b (p t) r s -> b p t (r s)", t=C_TILES)
    out_rows = out.rearrange("b (p t) r s -> b p t (r s)", t=C_TILES)

    with ExitStack() as ctx:
        const = ctx.enter_context(tc.tile_pool(name="const", bufs=1))
        rows = ctx.enter_context(tc.tile_pool(name="rows", bufs=ROW_BUFS))
        image = ctx.enter_context(tc.tile_pool(name="image", bufs=BATCH))
        work = ctx.enter_context(tc.tile_pool(name="work", bufs=2))
        stats = ctx.enter_context(tc.tile_pool(name="stats", bufs=4))
        packed = ctx.enter_context(tc.tile_pool(name="packed", bufs=2))
        turned = ctx.enter_context(tc.psum_pool(name="turned", bufs=4))
        sums = ctx.enter_context(tc.psum_pool(name="sums", bufs=4))

        identity = const.tile([P, P], F32, name="identity")
        make_identity(nc, identity[:])
        identity_bf16 = const.tile([P, P], BF16, name="identity_bf16")
        make_identity(nc, identity_bf16[:])
        gamma_bf16 = const.tile([P, 1], BF16, name="gamma_bf16")
        gamma_f32 = const.tile([P, 1], F32, name="gamma_f32")

        sim_tiles, fg_tiles, bg_tiles, x_tiles = {}, {}, {}, {}
        statistics = {}
        masked = {}
        scaled = {}
        pending = {}

        def empty(key):
            for target, source in pending.pop(key):
                nc.scalar.copy(out=target, in_=source)

        added = {}
        a_grouped = {}
        a_packed = {}
        x_grouped = {}
        x_packed = {}
        contexts = {}
        results = {}
        gated = {}

        def load_rows(k, tiles, source, name):
            tiles[k] = rows.tile([P, TILES, PIXELS], BF16, name=name)
            if k > 0:
                nc.sync.dma_start(out=tiles[k][:], in_=source[k, :, :, :])
            else:
                for j in range(TILES):
                    nc.sync.dma_start(out=tiles[k][:, j, :], in_=source[k, :, j, :])

        def load_sim(k):
            load_rows(k, sim_tiles, sim_rows, "sim_t")

        def load_fg(k):
            load_rows(k, fg_tiles, fg_rows, "fg_t")

        def load_bg(k):
            load_rows(k, bg_tiles, bg_rows, "bg_t")

        def load_channels(b, half):
            if half == 0:
                x_tiles[b] = image.tile([P, C_TILES, PIXELS], BF16, name="x_t")
            ts = slice(half * C_TILES // 2, (half + 1) * C_TILES // 2)
            nc.sync.dma_start(out=x_tiles[b][:, ts, :], in_=x_rows[b, :, ts, :])

        def by_word(row):
            return row.rearrange("n (g k t) -> n g k t", k=P, t=PACK)

        def into_blocks(blocks):
            return blocks.rearrange("n (g t) k -> n g k t", t=PACK)

        def minimum(k, j):
            if j == 0:
                statistics[k] = [
                    stats.tile([P, TILES], F32, name=name) for name in ("lowest", "total", "divisor", "inverse")
                ]
            unread = work.tile([P, PIXELS], BF16, name="unread")
            nc.vector.tensor_scalar(
                out=unread[:],
                in0=sim_tiles[k][:, j, :],
                scalar1=1.0,
                scalar2=None,
                op0=ALU.mult,
                op1=ALU.min,
                accum_out=statistics[k][0][:, j : j + 1],
            )

        def mask(k, j):
            lowest, total = statistics[k][0], statistics[k][1]
            x1 = work.tile([P, PIXELS], F32, name="x1", bufs=4)
            nc.vector.scalar_tensor_tensor(
                out=x1[:],
                in0=sim_tiles[k][:, j, :],
                scalar=lowest[:, j : j + 1],
                in1=fg_tiles[k][:, j, :],
                op0=ALU.subtract,
                op1=ALU.mult,
                accum_out=total[:, j : j + 1],
            )
            masked[k, j] = x1

        def divisor(k):
            nc.gpsimd.tensor_scalar_add(out=statistics[k][2][:], in0=statistics[k][1][:], scalar1=EPS)

        def invert(k):
            nc.vector.reciprocal(out=statistics[k][3][:], in_=statistics[k][2][:])
            a_grouped[k] = packed.tile(
                [P, PASSES, UNIT, PACK], BF16, name="a_grouped", align_bytes=64, bufs=LAG
            )

        def turn_words(source, grouped_words):
            words = source.bitcast(F32)
            bank = turned.tile([P, PASSES, PLANES, P], F32, name="bank")
            for g in range(PASSES):
                for u in range(PLANES):
                    base = g * PLANES * P
                    nc.tensor.transpose(
                        bank[:, g, u, :], words[:, base + u : base + PLANES * P : PLANES], identity[:]
                    )
            return [(grouped_words, bank[:].rearrange("k g u r -> k g r u"))]

        def turn_channel(b, t):
            quad, i = divmod(t, QUAD)
            if i == 0:
                x_grouped[b, quad] = packed.tile([P, QUAD, PASSES, P, PACK], BF16, name="x_grouped", align_bytes=64)
            x_words = x_grouped[b, quad][:].bitcast(F32)
            pending["x", b, t] = turn_words(x_tiles[b][:, t, :], x_words[:, i, :, :, :])

        def quantise_channels(b, quad):
            if quad == 0:
                x_codes = image.tile([P, C_TILES, PASSES, P], U32, name="x_codes", align_bytes=64)
                x_scales = image.tile([P, C_TILES, PASSES, P], U8, name="x_scales", align_bytes=64)
                x_packed[b] = (x_codes, x_scales)
            x_codes, x_scales = x_packed[b]
            cs = slice(QUAD * quad, QUAD * (quad + 1))
            nc.vector.quantize_mx(
                out=x_codes[:, cs, :, :].rearrange("k t g c -> k (t g c)").bitcast(FP8X4),
                scales=x_scales[:, cs, :, :].rearrange("k t g c -> k (t g c)"),
                in_=x_grouped[b, quad][:].rearrange("k t g c v -> k (t g c v)"),
            )

        def scale(k, j):
            blocks = work.tile([P, PASSES * PACK, P], F32, name="blocks", bufs=3)
            nc.scalar.activation(
                out=into_blocks(blocks[:]),
                in_=by_word(masked[k, j][:]),
                func=ACT.Copy,
                scale=statistics[k][3][:, j : j + 1],
            )
            scaled[k, j] = blocks

        def turn_sum(k, j):
            banks = [turned.tile([P, PACK, P], F32, name="bank") for g in range(PASSES)]
            for g in range(PASSES):
                for t in range(PACK):
                    nc.tensor.matmul(
                        out=banks[g][:, t, :],
                        lhsT=bg_tiles[k][:, j, g * K_PASS + t : (g + 1) * K_PASS : PACK],
                        rhs=identity_bf16[:],
                        start=(t == 0),
                        stop=False,
                    )
            for g in range(PASSES):
                for t in range(PACK):
                    nc.tensor.matmul(
                        out=banks[g][:, t, :],
                        lhsT=scaled[k, j][:, g * PACK + t, :],
                        rhs=identity[:],
                        is_transpose=True,
                        start=False,
                        stop=(t == PACK - 1),
                    )
            pending["a", k, j] = [
                (a_grouped[k][:, g, j * P : (j + 1) * P, :], banks[g][:].rearrange("k t r -> k r t"))
                for g in range(PASSES)
            ]

        def add_on_vector(k, j):
            a_rows = work.tile([P, PIXELS], BF16, name="a_rows")
            nc.vector.scalar_tensor_tensor(
                out=a_rows[:],
                in0=masked[k, j][:],
                scalar=statistics[k][3][:, j : j + 1],
                in1=bg_tiles[k][:, j, :],
                op0=ALU.mult,
                op1=ALU.add,
            )
            added[k, j] = a_rows

        def turn_rows(k, j):
            a_words = a_grouped[k][:].bitcast(F32)
            pending["a", k, j] = turn_words(added[k, j][:], a_words[:, :, j * P : (j + 1) * P, :])

        def quantise_rows(k):
            a_codes = packed.tile([P, PASSES, UNIT], U32, name="a_codes", align_bytes=64)
            a_scales = packed.tile([P, PASSES, UNIT], U8, name="a_scales", align_bytes=64)
            nc.vector.quantize_mx(
                out=a_codes[:].rearrange("k g n -> k (g n)").bitcast(FP8X4),
                scales=a_scales[:].rearrange("k g n -> k (g n)"),
                in_=a_grouped[k][:].rearrange("k g n v -> k (g n v)"),
            )
            a_packed[k] = (a_codes, a_scales)

        def multiply(k, c_pair):
            x_codes, x_scales = x_packed[k // IMAGE_UNITS]
            a_codes, a_scales = a_packed[k]
            context = sums.tile([P, PAIR, UNIT], F32, name="context")
            for i in range(PAIR):
                t = PAIR * c_pair + i
                for g in range(PASSES):
                    nc.tensor.matmul_mx(
                        out=context[:, i, :],
                        lhsT=x_codes[:, t, g, :].bitcast(FP8X4),
                        lhsT_scale=x_scales[:, t, g, :],
                        rhs=a_codes[:, g, :].bitcast(FP8X4),
                        rhs_scale=a_scales[:, g, :],
                        start=(g == 0),
                        stop=(g == PASSES - 1),
                    )
            contexts[k, c_pair] = context

        def gpsimd_pairs(k):
            return (0,) if k <= IMAGE_UNITS + 1 else ()

        def gate(k, c_pair):
            part = work.tile([P, PAIR, UNIT], F32, name="gated", bufs=3)
            nc.scalar.activation(out=part[:], in_=contexts[k, c_pair][:], func=ACT.Copy, scale=gamma_f32[:, 0:1])
            gated[k, c_pair] = part

        def finish(k, c_pair):
            b, s = divmod(k, IMAGE_UNITS)
            part = k % STORE_UNITS
            if c_pair == 0 and part == 0:
                result = work.tile([P, C_TILES, STORE_UNITS * UNIT], F32, name="result")
                results.update({k + i: result for i in range(STORE_UNITS)})
            result = results[k]
            cs = slice(PAIR * c_pair, PAIR * (c_pair + 1))
            pixels = slice(s * UNIT, (s + 1) * UNIT)
            columns = slice(part * UNIT, (part + 1) * UNIT)
            if (k, c_pair) in gated:
                nc.gpsimd.tensor_tensor(
                    out=result[:, cs, columns], in0=gated[k, c_pair][:], in1=x_tiles[b][:, cs, pixels], op=ALU.add
                )
            else:
                nc.vector.scalar_tensor_tensor(
                    out=result[:, cs, columns],
                    in0=contexts[k, c_pair][:],
                    scalar=gamma_bf16[:, 0:1],
                    in1=x_tiles[b][:, cs, pixels],
                    op0=ALU.mult,
                    op1=ALU.add,
                )

        def store(k, first, pairs):
            b, s = divmod(k, IMAGE_UNITS)
            part = k % STORE_UNITS
            ts = slice(PAIR * first, PAIR * (first + pairs))
            if b == BATCH - 1:
                columns = slice(part * UNIT, (part + 1) * UNIT)
                pixels = slice(s * UNIT, (s + 1) * UNIT)
            elif part == STORE_UNITS - 1:
                columns = slice(0, STORE_UNITS * UNIT)
                pixels = slice((s + 1 - STORE_UNITS) * UNIT, (s + 1) * UNIT)
            else:
                return
            nc.sync.dma_start(out=out_rows[b, :, ts, pixels], in_=results[k][:, ts, columns])

        def load_unit(k):
            load_sim(k)
            load_fg(k)
            load_bg(k)

        load_sim(0)
        load_fg(0)
        load_sim(1)
        load_bg(0)
        load_channels(0, 0)
        load_fg(1)
        load_channels(0, 1)
        load_sim(2)
        load_fg(2)
        load_bg(1)
        nc.sync.dma_start(out=gamma_bf16[:], in_=gamma.partition_broadcast(P))
        load_sim(3)
        load_fg(3)
        load_bg(2)
        load_channels(1, 0)
        load_sim(4)
        load_fg(4)
        load_channels(1, 1)
        load_bg(3)
        load_bg(4)
        load_sim(5)
        load_fg(5)
        load_bg(5)

        turn_steps = {
            0: [(0, t) for t in range(0, 4)],
            1: [(0, t) for t in range(4, 8)],
            3: [(1, 0), (1, 1)],
            4: [(1, 2), (1, 3)],
            5: [(1, t) for t in range(4, 8)],
        }
        quantise_steps = {1: [(0, 0)], 2: [(0, 1)], 5: [(1, 0)], 6: [(1, 1)]}

        with tc.manual_schedule(engines={ENGINE.PE, ENGINE.DVE, ENGINE.Activation, ENGINE.Pool}):
            for j in range(TILES):
                minimum(0, j)
            for k in range(UNITS + LAG - 1):
                fresh = k if k < UNITS else None
                turning = k - 1 if 1 <= k <= UNITS else None
                packed_now = k - 2 if 2 <= k < UNITS else None
                late = k - LAG if LAG <= k < UNITS else None
                drained = k - LAG + 1 if k >= UNITS - 1 else None
                draining = drained is not None
                if late is not None:
                    for c_pair in range(C_PAIRS):
                        multiply(late, c_pair)
                if fresh is not None:
                    mask(fresh, 0)
                    if draining:
                        quantise_rows(packed_now)
                    mask(fresh, 1)
                if turning in VECTOR_UNITS:
                    for j in range(TILES):
                        turn_rows(turning, j)
                        empty(("a", turning, j))
                elif turning is not None:
                    for j in range(TILES):
                        scale(turning, j)
                    if late is not None:
                        for c_pair in gpsimd_pairs(late):
                            gate(late, c_pair)
                if k == LAG - 1:
                    nc.scalar.copy(out=gamma_f32[:], in_=gamma_bf16[:])
                if fresh is not None:
                    divisor(fresh)
                if turning is not None and turning not in VECTOR_UNITS:
                    for j in range(TILES):
                        turn_sum(turning, j)
                        empty(("a", turning, j))
                for b, t in turn_steps.get(k, []):
                    turn_channel(b, t)
                for b, t in turn_steps.get(k, []):
                    empty(("x", b, t))
                if late is not None:
                    finish(late, 0)
                    finish(late, 1)
                    store(late, 0, 2)
                    finish(late, 2)
                    invert(fresh)
                    finish(late, 3)
                    store(late, 2, 2)
                if packed_now is not None and not draining:
                    quantise_rows(packed_now)
                for b, quad in quantise_steps.get(k, []):
                    quantise_channels(b, quad)
                if k + 1 < UNITS:
                    for j in range(TILES):
                        minimum(k + 1, j)
                if fresh is not None and late is None:
                    invert(fresh)
                if fresh in VECTOR_UNITS:
                    for j in range(TILES):
                        add_on_vector(fresh, j)
                if draining:
                    last = drained == UNITS - 1
                    for c_pair in range(C_PAIRS):
                        multiply(drained, c_pair)
                    for c_pair in gpsimd_pairs(drained):
                        gate(drained, c_pair)
                    for c_pair in range(C_PAIRS):
                        finish(drained, c_pair)
                        if last:
                            store(drained, c_pair, 1)
                        elif c_pair % 2 == 1:
                            store(drained, c_pair - 1, 2)
                        if c_pair == 1 and not last:
                            quantise_rows(drained + 1)
                if k > 0 and k - 1 + ROW_BUFS < UNITS:
                    load_unit(k - 1 + ROW_BUFS)
